import numpy as np
import ml_dtypes


def mxq(x, axis, fmt="e4m3"):
    dtype, down = {"e4m3": (ml_dtypes.float8_e4m3fn, 7), "e5m2": (ml_dtypes.float8_e5m2, 14)}[fmt]
    v = np.moveaxis(np.asarray(x, np.float32).astype(ml_dtypes.bfloat16).astype(np.float64), axis, -1)
    blocks = v.reshape(v.shape[:-1] + (-1, 32))
    amax = np.abs(blocks).max(-1, keepdims=True)
    byte = np.maximum(np.where(amax > 0, np.frexp(amax)[1] - 1 + 127, 0) - down, 1)
    scale = np.exp2(byte - 127.0)
    codes = (blocks / scale).astype(np.float32).astype(dtype).astype(np.float64)
    return np.moveaxis((codes * scale).reshape(v.shape), -1, axis)


WIDE = False


def mx_kscale(k):
    if not WIDE:
        return np.ones(k)
    levels = np.array([20, -20, 10, -10, 0])
    a = np.random.permutation(np.resize(levels, k // 512 * 4)).reshape(k // 512, 4)
    idx = np.arange(k)
    return np.exp2(a[idx // 512, idx % 128 // 32])


BF16 = ml_dtypes.bfloat16


def bf(x):
    return np.asarray(x, np.float32).astype(BF16)


def f64(x):
    return np.asarray(x).astype(np.float64)


B, T, HS, WS, C, HN, D = 1, 8, 8, 8, 2048, 16, 128
N = T * HS * WS
E = HN * D
EPS = 1e-6
BASE = 10000.0


def axis_angles(n, dim):
    f = 1.0 / BASE ** (np.arange(0, dim, 2)[: dim // 2] / dim)
    return np.repeat(np.arange(n)[:, None] * f[None, :], 2, axis=-1)


def rope_angles():
    dim_t = D - 4 * (D // 6)
    dim_h = 2 * (D // 6)
    dim_w = 2 * (D // 6)
    at = np.broadcast_to(axis_angles(T, dim_t)[:, None, None, :], (T, HS, WS, dim_t))
    ah = np.broadcast_to(axis_angles(HS, dim_h)[None, :, None, :], (T, HS, WS, dim_h))
    aw = np.broadcast_to(axis_angles(WS, dim_w)[None, None, :, :], (T, HS, WS, dim_w))
    return np.concatenate([at, ah, aw], axis=-1).reshape(N, D)


def rotate_half(v):
    p = v.reshape(v.shape[:-1] + (v.shape[-1] // 2, 2))
    return np.stack((-p[..., 1], p[..., 0]), axis=-1).reshape(v.shape)


def setup_inputs():
    s = mx_kscale(N)
    x0 = bf(np.random.standard_normal((B, N, C)))
    w = bf(np.random.standard_normal((E, C)) / np.sqrt(C))
    b = bf(np.random.standard_normal(E) * 0.3)
    norm_w = bf(1.0 + 0.1 * np.random.standard_normal(D))
    g = bf(np.random.standard_normal((B, HN, N, D)) * np.exp2(np.random.randint(-12, 1, (B, 1, N, 1))) / s[None, None, :, None])
    y = f64(x0) @ f64(w).T + f64(b)
    return {"x": bf(f64(x0) * s[None, :, None]), "w": w, "b": b, "norm_w": norm_w,
            "y": np.asarray(y, np.float32), "grad_out": g}


def reference(x, w, b, norm_w, y, grad_out):
    g = f64(grad_out)
    a = rope_angles()
    du = g * np.cos(a) - rotate_half(g) * np.sin(a)
    dn = du * f64(norm_w)
    yh = f64(y).reshape(B, N, HN, D).transpose(0, 2, 1, 3)
    r = 1.0 / np.sqrt(np.mean(yh * yh, axis=-1, keepdims=True) + EPS)
    dyh = r * (dn - yh * r * r * np.mean(dn * yh, axis=-1, keepdims=True))
    dy = dyh.transpose(0, 2, 1, 3).reshape(B * N, E)
    x2 = f64(x).reshape(B * N, C)
    return mxq(dy, 0, "e5m2").T @ mxq(x2, 0, "e4m3")

@@ -1,0 +1,298 @@
+import math
+
+import concourse.mybir as mybir
+
+F32 = mybir.dt.float32
+BF16 = mybir.dt.bfloat16
+I32 = mybir.dt.int32
+U32 = mybir.dt.uint32
+U8 = mybir.dt.uint8
+E4M3_X4 = mybir.dt.float8_e4m3fn_x4
+E5M2_X4 = mybir.dt.float8_e5m2_x4
+ALU = mybir.AluOpType
+ACT = mybir.ActivationFunctionType
+
+P = 128
+PACK = 4
+TOKENS = P * PACK
+HEADS = 16
+D = 128
+PAIRS = D // 2
+E = HEADS * D
+C = 2048
+EPS = 1e-6
+BASE = 10000.0
+DIM_T = D - 4 * (D // 6)
+DIM_HW = 2 * (D // 6)
+PAIRS_T = DIM_T // 2
+PAIRS_HW = DIM_HW // 2
+
+BANK = 512
+X_CHUNKS = C // BANK
+STORE = 2 * BANK
+QUAD = 4
+QUADS = HEADS // QUAD
+NORM_LEAD = QUAD + 1
+
+FLOPS = 2 * TOKENS * E * C
+BYTES = 2 * TOKENS * C + 2 * D + 4 * TOKENS * E + 2 * TOKENS * E + 4 * E * C
+
+
+def tile_attention_pa_v_kernel(tc, x, w, b, norm_w, y, grad_out, out):
+    nc = tc.nc
+    x_rows = x.flatten_outer_dims().rearrange("(p j) c -> p j c", j=PACK)
+    y_rows = y.flatten_outer_dims().rearrange("(p j) e -> p j e", j=PACK)
+    g_rows = grad_out.flatten_outer_dims().rearrange("(h p j) d -> p h (j d)", h=HEADS, j=PACK)
+
+    with tc.tile_pool(name="keep", bufs=1) as keep, tc.tile_pool(name="work", bufs=3) as work, tc.psum_pool(
+        name="psum", bufs=8
+    ) as psum:
+        gain = keep.tile([P, D], BF16)
+        nc.scalar.dma_start(out=gain[:], in_=norm_w.partition_broadcast(P))
+
+        x_raw = [keep.tile([P, PACK, BANK], BF16, name="x_raw%d" % c) for c in range(X_CHUNKS)]
+        y_quad = [keep.tile([P, PACK, QUAD * D], F32, name="y_quad%d" % q) for q in range(QUADS)]
+        g_quad = [keep.tile([P, QUAD, PACK, D], BF16, name="g_quad%d" % q) for q in range(QUADS)]
+
+        def load_x(c):
+            nc.sync.dma_start(out=x_raw[c][:], in_=x_rows[:, :, c * BANK : (c + 1) * BANK])
+
+        def load_y(q):
+            nc.sync.dma_start(out=y_quad[q][:], in_=y_rows[:, :, q * QUAD * D : (q + 1) * QUAD * D])
+
+        def load_g(q):
+            nc.sync.dma_start(
+                out=g_quad[q][:].rearrange("p h j d -> p h (j d)"), in_=g_rows[:, q * QUAD : (q + 1) * QUAD, :]
+            )
+
+        load_x(0)
+        load_x(1)
+        load_y(0)
+        load_x(2)
+        load_x(3)
+        load_g(0)
+        for q in range(1, QUADS):
+            load_y(q)
+            load_g(q)
+
+        token = keep.tile([P, PACK], I32)
+        nc.gpsimd.iota(token[:], pattern=[[1, PACK]], base=0, channel_multiplier=PACK)
+        grid_int = keep.tile([P, 3, PACK], I32)
+        nc.vector.tensor_single_scalar(out=grid_int[:, 0, :], in_=token[:], scalar=6, op=ALU.arith_shift_right)
+        nc.vector.tensor_scalar(
+            out=grid_int[:, 1, :],
+            in0=token[:],
+            scalar1=3,
+            scalar2=7,
+            op0=ALU.arith_shift_right,
+            op1=ALU.bitwise_and,
+        )
+        nc.vector.tensor_single_scalar(out=grid_int[:, 2, :], in_=token[:], scalar=7, op=ALU.bitwise_and)
+        grid = keep.tile([P, 3, PACK], F32)
+        nc.vector.tensor_copy(out=grid[:], in_=grid_int[:])
+
+        turn = keep.tile([P, 2, PACK, PAIRS], F32)
+        for k in range(PAIRS_T):
+            nc.vector.tensor_scalar_mul(out=turn[:, 0, :, k], in0=grid[:, 0, :], scalar1=BASE ** (-2.0 * k / DIM_T))
+        turn_hw = turn[:, 0, :, PAIRS_T:].rearrange("p j (a k) -> p j a k", a=2)
+        grid_hw = grid[:, 1:3, :].rearrange("p a j -> p j a")
+        for k in range(PAIRS_HW):
+            nc.vector.tensor_scalar_mul(out=turn_hw[:, :, :, k], in0=grid_hw, scalar1=BASE ** (-2.0 * k / DIM_HW))
+        nc.vector.tensor_scalar_add(out=turn[:, 1], in0=turn[:, 0], scalar1=0.5 * math.pi)
+        full_turn = keep.tile([P, 2, PACK, PAIRS], F32)
+        nc.vector.tensor_scalar(
+            out=full_turn[:], in0=turn[:], scalar1=math.pi, scalar2=2.0 * math.pi, op0=ALU.is_gt, op1=ALU.mult
+        )
+        wrapped = keep.tile([P, 2, PACK, PAIRS], F32)
+        nc.vector.tensor_sub(out=wrapped[:], in0=turn[:], in1=full_turn[:])
+        sin_cos = keep.tile([P, 2, PACK, PAIRS], F32)
+        nc.scalar.activation(out=sin_cos[:], in_=wrapped[:], func=ACT.Sin)
+
+        table = keep.tile([P, 2, PACK, D], F32)
+        gain_pairs = gain[:].rearrange("p (m e) -> p m e", e=2)
+        nc.vector.tensor_tensor(
+            out=table[:, 0].rearrange("p j (m e) -> p j m e", e=2),
+            in0=sin_cos[:, 1].unsqueeze(3).to_broadcast([P, PACK, PAIRS, 2]),
+            in1=gain_pairs.unsqueeze(1).to_broadcast([P, PACK, PAIRS, 2]),
+            op=ALU.mult,
+        )
+        cross = table[:, 1].rearrange("p j (m e) -> p j m e", e=2)
+        for e in range(2):
+            nc.vector.tensor_tensor(
+                out=cross[:, :, :, e],
+                in0=sin_cos[:, 0],
+                in1=gain_pairs[:, :, 1 - e].unsqueeze(1).to_broadcast([P, PACK, PAIRS]),
+                op=ALU.mult,
+            )
+
+        eps = keep.tile([P, 1], F32)
+        nc.vector.memset(eps[:], EPS)
+
+        x_grouped = [keep.tile([P, BANK, PACK], BF16, name="x_grouped%d" % c, align_bytes=64) for c in range(X_CHUNKS)]
+        x_codes = [keep.tile([P, BANK], U32, name="x_codes%d" % c, align_bytes=64) for c in range(X_CHUNKS)]
+        x_scales = [keep.tile([P, BANK], U8, name="x_scales%d" % c, align_bytes=64) for c in range(X_CHUNKS)]
+
+        def regroup_x(engine_copy, c):
+            engine_copy(out=x_grouped[c][:], in_=x_raw[c][:].rearrange("p j c -> p c j"))
+
+        def quantise_x(c):
+            nc.vector.quantize_mx(
+                out=x_codes[c][:].bitcast(E4M3_X4),
+                scales=x_scales[c][:],
+                in_=x_grouped[c][:].rearrange("p c j -> p (c j)"),
+            )
+
+        square_sum = [keep.tile([P, QUAD, PACK], F32, name="square_sum%d" % q) for q in range(QUADS)]
+        rms = [keep.tile([P, QUAD, PACK], F32, name="rms%d" % q) for q in range(QUADS)]
+        r = [keep.tile([P, QUAD, PACK], F32, name="r%d" % q) for q in range(QUADS)]
+        r_squared = [keep.tile([P, QUAD, PACK], F32, name="r_squared%d" % q) for q in range(QUADS)]
+
+        def y_of(h, j):
+            return y_quad[h // QUAD][:, j, (h % QUAD) * D : (h % QUAD + 1) * D]
+
+        def sum_squares(h):
+            squares = work.tile([P, PACK, D], F32)
+            for j in range(PACK):
+                nc.scalar.activation(
+                    out=squares[:, j, :],
+                    in_=y_of(h, j),
+                    func=ACT.Square,
+                    accum_out=square_sum[h // QUAD][:, h % QUAD, j : j + 1],
+                )
+
+        def root(q):
+            nc.scalar.activation(out=rms[q][:], in_=square_sum[q][:], func=ACT.Sqrt, scale=1.0 / D, bias=eps[:, 0:1])
+
+        def invert(q):
+            nc.vector.reciprocal(out=r[q][:], in_=rms[q][:])
+            nc.vector.tensor_mul(out=r_squared[q][:], in0=r[q][:], in1=r[q][:])
+
+        products, dn, coefficient, dy_rows, dy_grouped, dy_codes, dy_scales = {}, {}, {}, {}, {}, {}, {}
+
+        def rotate_products(h):
+            tile = work.tile([P, 2, PACK, D], F32, name="products")
+            for j in range(PACK):
+                nc.vector.scalar_tensor_tensor(
+                    out=tile[:, :, j, :],
+                    in0=g_quad[h // QUAD][:, h % QUAD, j, :].unsqueeze(1).to_broadcast([P, 2, D]),
+                    scalar=r[h // QUAD][:, h % QUAD, j : j + 1],
+                    in1=table[:, :, j, :],
+                    op0=ALU.mult,
+                    op1=ALU.mult,
+                )
+            products[h] = tile
+
+        def rotate_sums(h):
+            tile = work.tile([P, PACK, 2, PAIRS], F32, name="dn")
+            own = products[h][:, 0].rearrange("p j (m e) -> p j m e", e=2)
+            other = products[h][:, 1].rearrange("p j (m e) -> p j m e", e=2)
+            nc.vector.tensor_tensor(out=tile[:, :, 0, :], in0=own[:, :, :, 0], in1=other[:, :, :, 1], op=ALU.add)
+            nc.vector.tensor_tensor(out=tile[:, :, 1, :], in0=own[:, :, :, 1], in1=other[:, :, :, 0], op=ALU.subtract)
+            dn[h] = tile
+
+        def project_dots(h):
+            dot = work.tile([P, PACK], F32, name="dot")
+            terms = work.tile([P, PACK, D], F32, name="terms")
+            for j in range(PACK):
+                nc.vector.scalar_tensor_tensor(
+                    out=terms[:, j, :].rearrange("p (m e) -> p m e", e=2),
+                    in0=dn[h][:, j].rearrange("p e m -> p m e"),
+                    scalar=1.0,
+                    in1=y_of(h, j).rearrange("p (m e) -> p m e", e=2),
+                    op0=ALU.mult,
+                    op1=ALU.mult,
+                    accum_out=dot[:, j : j + 1],
+                )
+            tile = work.tile([P, PACK], F32, name="coefficient")
+            nc.vector.scalar_tensor_tensor(
+                out=tile[:],
+                in0=dot[:],
+                scalar=-1.0 / D,
+                in1=r_squared[h // QUAD][:, h % QUAD, :],
+                op0=ALU.mult,
+                op1=ALU.mult,
+            )
+            coefficient[h] = tile
+
+        def project(h):
+            tile = work.tile([P, PACK, D], BF16, name="dy_rows")
+            for j in range(PACK):
+                nc.vector.scalar_tensor_tensor(
+                    out=tile[:, j, :].rearrange("p (m e) -> p m e", e=2),
+                    in0=y_of(h, j).rearrange("p (m e) -> p m e", e=2),
+                    scalar=coefficient[h][:, j : j + 1],
+                    in1=dn[h][:, j].rearrange("p e m -> p m e"),
+                    op0=ALU.mult,
+                    op1=ALU.add,
+                )
+            dy_rows[h] = tile
+
+        def regroup_dy(h):
+            tile = work.tile([P, D, PACK], BF16, name="dy_grouped", align_bytes=64)
+            nc.scalar.copy(out=tile[:], in_=dy_rows[h][:].rearrange("p j d -> p d j"))
+            dy_grouped[h] = tile
+
+        def quantise_dy(h):
+            codes = work.tile([P, D], U32, name="dy_codes", align_bytes=64)
+            scales = work.tile([P, D], U8, name="dy_scales", align_bytes=64)
+            nc.vector.quantize_mx(
+                out=codes[:].bitcast(E5M2_X4), scales=scales[:], in_=dy_grouped[h][:].rearrange("p d j -> p (d j)")
+            )
+            dy_codes[h] = codes
+            dy_scales[h] = scales
+
+        def multiply_and_store(h):
+            for half in range(C // STORE):
+                result = work.tile([P, STORE], F32, name="result", bufs=4)
+                for i in range(STORE // BANK):
+                    c = half * (STORE // BANK) + i
+                    acc = psum.tile([P, BANK], F32, name="acc")
+                    nc.tensor.matmul_mx(
+                        out=acc[:],
+                        lhsT=dy_codes[h][:].bitcast(E5M2_X4),
+                        lhsT_scale=dy_scales[h][:],
+                        rhs=x_codes[c][:].bitcast(E4M3_X4),
+                        rhs_scale=x_scales[c][:],
+                        start=True,
+                        stop=True,
+                    )
+                    nc.scalar.copy(out=result[:, i * BANK : (i + 1) * BANK], in_=acc[:])
+                nc.sync.dma_start(
+                    out=out[h * D : (h + 1) * D, half * STORE : (half + 1) * STORE], in_=result[:]
+                )
+
+        regroup_x(nc.vector.tensor_copy, 0)
+        regroup_x(nc.vector.tensor_copy, 1)
+        quantise_x(0)
+        quantise_x(1)
+        for h in range(QUAD):
+            sum_squares(h)
+        root(0)
+        invert(0)
+        regroup_x(nc.scalar.copy, 2)
+        regroup_x(nc.scalar.copy, 3)
+        for h in range(QUAD, NORM_LEAD):
+            sum_squares(h)
+
+        for k in range(HEADS + 2):
+            if k < HEADS:
+                rotate_products(k)
+            if 1 <= k <= HEADS:
+                project(k - 1)
+                regroup_dy(k - 1)
+            if k < HEADS:
+                rotate_sums(k)
+            if k < 2:
+                quantise_x(2 + k)
+            else:
+                quantise_dy(k - 2)
+            if k < HEADS:
+                project_dots(k)
+            ahead = k + NORM_LEAD
+            if ahead < HEADS:
+                sum_squares(ahead)
+                if ahead % QUAD == QUAD - 1:
+                    root(ahead // QUAD)
+                    invert(ahead // QUAD)
+            if k >= 2:
+                multiply_and_store(k - 2)

@@ -1,6 +1,7 @@
 import math
 
 import concourse.mybir as mybir
+from concourse.masks import make_identity
 
 F32 = mybir.dt.float32
 BF16 = mybir.dt.bfloat16
@@ -32,10 +33,18 @@ X_CHUNKS = C // BANK
 STORE = 2 * BANK
 QUAD = 4
 QUADS = HEADS // QUAD
-NORM_LEAD = QUAD + 1
+NORM_LEAD = 2 * QUAD
+RUN = 4
 
 FLOPS = 2 * TOKENS * E * C
 BYTES = 2 * TOKENS * C + 2 * D + 4 * TOKENS * E + 2 * TOKENS * E + 4 * E * C
+
+
+def regroup(copy, grouped, rows):
+    copy(
+        out=grouped.rearrange("p (c i) j -> p c j i", i=RUN),
+        in_=rows.rearrange("p j (c i) -> p c j i", i=RUN),
+    )
 
 
 def tile_attention_pa_v_kernel(tc, x, w, b, norm_w, y, grad_out, out):
@@ -45,8 +54,8 @@ def tile_attention_pa_v_kernel(tc, x, w, b, norm_w, y, grad_out, out):
     g_rows = grad_out.flatten_outer_dims().rearrange("(h p j) d -> p h (j d)", h=HEADS, j=PACK)
 
     with tc.tile_pool(name="keep", bufs=1) as keep, tc.tile_pool(name="work", bufs=3) as work, tc.psum_pool(
-        name="psum", bufs=8
-    ) as psum:
+        name="psum", bufs=2
+    ) as psum, tc.manual_schedule():
         gain = keep.tile([P, D], BF16)
         nc.scalar.dma_start(out=gain[:], in_=norm_w.partition_broadcast(P))
 
@@ -68,15 +77,17 @@ def tile_attention_pa_v_kernel(tc, x, w, b, norm_w, y, grad_out, out):
         load_x(0)
         load_x(1)
         load_y(0)
+        load_g(0)
         load_x(2)
         load_x(3)
-        load_g(0)
         for q in range(1, QUADS):
             load_y(q)
             load_g(q)
 
         token = keep.tile([P, PACK], I32)
         nc.gpsimd.iota(token[:], pattern=[[1, PACK]], base=0, channel_multiplier=PACK)
+        identity = keep.tile([P, P], BF16)
+        make_identity(nc, identity[:])
         grid_int = keep.tile([P, 3, PACK], I32)
         nc.vector.tensor_single_scalar(out=grid_int[:, 0, :], in_=token[:], scalar=6, op=ALU.arith_shift_right)
         nc.vector.tensor_scalar(
@@ -90,50 +101,44 @@ def tile_attention_pa_v_kernel(tc, x, w, b, norm_w, y, grad_out, out):
         nc.vector.tensor_single_scalar(out=grid_int[:, 2, :], in_=token[:], scalar=7, op=ALU.bitwise_and)
         grid = keep.tile([P, 3, PACK], F32)
         nc.vector.tensor_copy(out=grid[:], in_=grid_int[:])
+        eps = keep.tile([P, 1], F32)
+        nc.vector.memset(eps[:], EPS)
 
         turn = keep.tile([P, 2, PACK, PAIRS], F32)
         for k in range(PAIRS_T):
-            nc.vector.tensor_scalar_mul(out=turn[:, 0, :, k], in0=grid[:, 0, :], scalar1=BASE ** (-2.0 * k / DIM_T))
-        turn_hw = turn[:, 0, :, PAIRS_T:].rearrange("p j (a k) -> p j a k", a=2)
+            nc.vector.tensor_scalar_mul(out=turn[:, 1, :, k], in0=grid[:, 0, :], scalar1=BASE ** (-2.0 * k / DIM_T))
+        turn_hw = turn[:, 1, :, PAIRS_T:].rearrange("p j (a k) -> p j a k", a=2)
         grid_hw = grid[:, 1:3, :].rearrange("p a j -> p j a")
         for k in range(PAIRS_HW):
             nc.vector.tensor_scalar_mul(out=turn_hw[:, :, :, k], in0=grid_hw, scalar1=BASE ** (-2.0 * k / DIM_HW))
-        nc.vector.tensor_scalar_add(out=turn[:, 1], in0=turn[:, 0], scalar1=0.5 * math.pi)
+        nc.vector.tensor_scalar_add(out=turn[:, 0], in0=turn[:, 1], scalar1=0.5 * math.pi)
         full_turn = keep.tile([P, 2, PACK, PAIRS], F32)
         nc.vector.tensor_scalar(
             out=full_turn[:], in0=turn[:], scalar1=math.pi, scalar2=2.0 * math.pi, op0=ALU.is_gt, op1=ALU.mult
         )
         wrapped = keep.tile([P, 2, PACK, PAIRS], F32)
         nc.vector.tensor_sub(out=wrapped[:], in0=turn[:], in1=full_turn[:])
-        sin_cos = keep.tile([P, 2, PACK, PAIRS], F32)
-        nc.scalar.activation(out=sin_cos[:], in_=wrapped[:], func=ACT.Sin)
+        cos_sin = keep.tile([P, 2, PACK, PAIRS], F32)
+        nc.scalar.activation(out=cos_sin[:], in_=wrapped[:], func=ACT.Sin)
 
-        table = keep.tile([P, 2, PACK, D], F32)
+        gains = keep.tile([P, 2, PAIRS, 2], F32)
         gain_pairs = gain[:].rearrange("p (m e) -> p m e", e=2)
-        nc.vector.tensor_tensor(
-            out=table[:, 0].rearrange("p j (m e) -> p j m e", e=2),
-            in0=sin_cos[:, 1].unsqueeze(3).to_broadcast([P, PACK, PAIRS, 2]),
-            in1=gain_pairs.unsqueeze(1).to_broadcast([P, PACK, PAIRS, 2]),
-            op=ALU.mult,
-        )
-        cross = table[:, 1].rearrange("p j (m e) -> p j m e", e=2)
-        for e in range(2):
+        nc.vector.tensor_copy(out=gains[:, 0], in_=gain_pairs)
+        nc.vector.tensor_copy(out=gains[:, 1, :, 0], in_=gain_pairs[:, :, 0])
+        nc.vector.tensor_scalar_mul(out=gains[:, 1, :, 1], in0=gain_pairs[:, :, 1], scalar1=-1.0)
+        table = keep.tile([P, 2, PACK, D], F32)
+
+        def build_table():
             nc.vector.tensor_tensor(
-                out=cross[:, :, :, e],
-                in0=sin_cos[:, 0],
-                in1=gain_pairs[:, :, 1 - e].unsqueeze(1).to_broadcast([P, PACK, PAIRS]),
+                out=table[:].rearrange("p k j (m e) -> p k j m e", e=2),
+                in0=cos_sin[:].unsqueeze(4).to_broadcast([P, 2, PACK, PAIRS, 2]),
+                in1=gains[:].unsqueeze(2).to_broadcast([P, 2, PACK, PAIRS, 2]),
                 op=ALU.mult,
             )
-
-        eps = keep.tile([P, 1], F32)
-        nc.vector.memset(eps[:], EPS)
 
         x_grouped = [keep.tile([P, BANK, PACK], BF16, name="x_grouped%d" % c, align_bytes=64) for c in range(X_CHUNKS)]
         x_codes = [keep.tile([P, BANK], U32, name="x_codes%d" % c, align_bytes=64) for c in range(X_CHUNKS)]
         x_scales = [keep.tile([P, BANK], U8, name="x_scales%d" % c, align_bytes=64) for c in range(X_CHUNKS)]
-
-        def regroup_x(engine_copy, c):
-            engine_copy(out=x_grouped[c][:], in_=x_raw[c][:].rearrange("p j c -> p c j"))
 
         def quantise_x(c):
             nc.vector.quantize_mx(
@@ -150,6 +155,9 @@ def tile_attention_pa_v_kernel(tc, x, w, b, norm_w, y, grad_out, out):
         def y_of(h, j):
             return y_quad[h // QUAD][:, j, (h % QUAD) * D : (h % QUAD + 1) * D]
 
+        def r_of(h, j):
+            return r[h // QUAD][:, h % QUAD, j : j + 1]
+
         def sum_squares(h):
             squares = work.tile([P, PACK, D], F32)
             for j in range(PACK):
@@ -159,140 +167,179 @@ def tile_attention_pa_v_kernel(tc, x, w, b, norm_w, y, grad_out, out):
                     func=ACT.Square,
                     accum_out=square_sum[h // QUAD][:, h % QUAD, j : j + 1],
                 )
-
-        def root(q):
-            nc.scalar.activation(out=rms[q][:], in_=square_sum[q][:], func=ACT.Sqrt, scale=1.0 / D, bias=eps[:, 0:1])
+            if h % QUAD == QUAD - 1:
+                q = h // QUAD
+                nc.scalar.activation(
+                    out=rms[q][:], in_=square_sum[q][:], func=ACT.Sqrt, scale=1.0 / D, bias=eps[:, 0:1]
+                )
 
         def invert(q):
             nc.vector.reciprocal(out=r[q][:], in_=rms[q][:])
             nc.vector.tensor_mul(out=r_squared[q][:], in0=r[q][:], in1=r[q][:])
 
-        products, dn, coefficient, dy_rows, dy_grouped, dy_codes, dy_scales = {}, {}, {}, {}, {}, {}, {}
+        swapped, own, other, dn, dot, coefficient, dy_rows, dy_grouped, dy_codes, dy_scales, acc = (
+            {},
+            {},
+            {},
+            {},
+            {},
+            {},
+            {},
+            {},
+            {},
+            {},
+            {},
+        )
 
-        def rotate_products(h):
-            tile = work.tile([P, 2, PACK, D], F32, name="products")
+        def swap_pairs(h):
+            bank = psum.tile([P, PACK, PAIRS, 2], F32, name="swapped")
+            pairs = g_quad[h // QUAD][:, h % QUAD].rearrange("p j (m e) -> p j m e", e=2)
+            for e in range(2):
+                nc.tensor.matmul(
+                    out=bank[:, :, :, e], lhsT=identity[:], rhs=pairs[:, :, :, 1 - e], start=True, stop=True
+                )
+            swapped[h] = bank
+
+        def rotate_own(h):
+            own[h] = work.tile([P, PACK, D], F32, name="own")
             for j in range(PACK):
                 nc.vector.scalar_tensor_tensor(
-                    out=tile[:, :, j, :],
-                    in0=g_quad[h // QUAD][:, h % QUAD, j, :].unsqueeze(1).to_broadcast([P, 2, D]),
-                    scalar=r[h // QUAD][:, h % QUAD, j : j + 1],
-                    in1=table[:, :, j, :],
+                    out=own[h][:, j, :],
+                    in0=g_quad[h // QUAD][:, h % QUAD, j, :],
+                    scalar=r_of(h, j),
+                    in1=table[:, 0, j, :],
                     op0=ALU.mult,
                     op1=ALU.mult,
                 )
-            products[h] = tile
 
-        def rotate_sums(h):
-            tile = work.tile([P, PACK, 2, PAIRS], F32, name="dn")
-            own = products[h][:, 0].rearrange("p j (m e) -> p j m e", e=2)
-            other = products[h][:, 1].rearrange("p j (m e) -> p j m e", e=2)
-            nc.vector.tensor_tensor(out=tile[:, :, 0, :], in0=own[:, :, :, 0], in1=other[:, :, :, 1], op=ALU.add)
-            nc.vector.tensor_tensor(out=tile[:, :, 1, :], in0=own[:, :, :, 1], in1=other[:, :, :, 0], op=ALU.subtract)
-            dn[h] = tile
+        def rotate_other(h):
+            other[h] = work.tile([P, PACK, D], F32, name="other")
+            for j in range(PACK):
+                nc.vector.scalar_tensor_tensor(
+                    out=other[h][:, j, :],
+                    in0=swapped[h][:, j].rearrange("p m e -> p (m e)"),
+                    scalar=r_of(h, j),
+                    in1=table[:, 1, j, :],
+                    op0=ALU.mult,
+                    op1=ALU.mult,
+                )
 
-        def project_dots(h):
-            dot = work.tile([P, PACK], F32, name="dot")
+        def rotate_sum(h):
+            dn[h] = work.tile([P, PACK, D], F32, name="dn")
+            nc.vector.tensor_add(out=dn[h][:], in0=own[h][:], in1=other[h][:])
+
+        def dots(h):
+            dot[h] = work.tile([P, PACK], F32, name="dot")
             terms = work.tile([P, PACK, D], F32, name="terms")
             for j in range(PACK):
                 nc.vector.scalar_tensor_tensor(
-                    out=terms[:, j, :].rearrange("p (m e) -> p m e", e=2),
-                    in0=dn[h][:, j].rearrange("p e m -> p m e"),
+                    out=terms[:, j, :],
+                    in0=dn[h][:, j, :],
                     scalar=1.0,
-                    in1=y_of(h, j).rearrange("p (m e) -> p m e", e=2),
+                    in1=y_of(h, j),
                     op0=ALU.mult,
                     op1=ALU.mult,
-                    accum_out=dot[:, j : j + 1],
+                    accum_out=dot[h][:, j : j + 1],
                 )
-            tile = work.tile([P, PACK], F32, name="coefficient")
+
+        def scale_dots(h):
+            coefficient[h] = work.tile([P, PACK], F32, name="coefficient")
             nc.vector.scalar_tensor_tensor(
-                out=tile[:],
-                in0=dot[:],
+                out=coefficient[h][:],
+                in0=dot[h][:],
                 scalar=-1.0 / D,
                 in1=r_squared[h // QUAD][:, h % QUAD, :],
                 op0=ALU.mult,
                 op1=ALU.mult,
             )
-            coefficient[h] = tile
 
-        def project(h):
-            tile = work.tile([P, PACK, D], BF16, name="dy_rows")
-            for j in range(PACK):
+        def project(h, tokens):
+            if h not in dy_rows:
+                dy_rows[h] = work.tile([P, PACK, D], BF16, name="dy_rows")
+            for j in tokens:
                 nc.vector.scalar_tensor_tensor(
-                    out=tile[:, j, :].rearrange("p (m e) -> p m e", e=2),
-                    in0=y_of(h, j).rearrange("p (m e) -> p m e", e=2),
+                    out=dy_rows[h][:, j, :],
+                    in0=y_of(h, j),
                     scalar=coefficient[h][:, j : j + 1],
-                    in1=dn[h][:, j].rearrange("p e m -> p m e"),
+                    in1=dn[h][:, j, :],
                     op0=ALU.mult,
                     op1=ALU.add,
                 )
-            dy_rows[h] = tile
 
         def regroup_dy(h):
-            tile = work.tile([P, D, PACK], BF16, name="dy_grouped", align_bytes=64)
-            nc.scalar.copy(out=tile[:], in_=dy_rows[h][:].rearrange("p j d -> p d j"))
-            dy_grouped[h] = tile
+            dy_grouped[h] = work.tile([P, D, PACK], BF16, name="dy_grouped", align_bytes=64)
+            regroup(nc.scalar.copy, dy_grouped[h][:], dy_rows[h][:])
 
         def quantise_dy(h):
-            codes = work.tile([P, D], U32, name="dy_codes", align_bytes=64)
-            scales = work.tile([P, D], U8, name="dy_scales", align_bytes=64)
+            dy_codes[h] = work.tile([P, D], U32, name="dy_codes", align_bytes=64)
+            dy_scales[h] = work.tile([P, D], U8, name="dy_scales", align_bytes=64)
             nc.vector.quantize_mx(
-                out=codes[:].bitcast(E5M2_X4), scales=scales[:], in_=dy_grouped[h][:].rearrange("p d j -> p (d j)")
+                out=dy_codes[h][:].bitcast(E5M2_X4),
+                scales=dy_scales[h][:],
+                in_=dy_grouped[h][:].rearrange("p d j -> p (d j)"),
             )
-            dy_codes[h] = codes
-            dy_scales[h] = scales
 
-        def multiply_and_store(h):
+        def multiply(h):
+            for c in range(X_CHUNKS):
+                acc[h, c] = psum.tile([P, BANK], F32, name="acc", bufs=6)
+                nc.tensor.matmul_mx(
+                    out=acc[h, c][:],
+                    lhsT=dy_codes[h][:].bitcast(E5M2_X4),
+                    lhsT_scale=dy_scales[h][:],
+                    rhs=x_codes[c][:].bitcast(E4M3_X4),
+                    rhs_scale=x_scales[c][:],
+                    start=True,
+                    stop=True,
+                )
+
+        def empty_and_store(h, copy):
             for half in range(C // STORE):
                 result = work.tile([P, STORE], F32, name="result", bufs=4)
                 for i in range(STORE // BANK):
-                    c = half * (STORE // BANK) + i
-                    acc = psum.tile([P, BANK], F32, name="acc")
-                    nc.tensor.matmul_mx(
-                        out=acc[:],
-                        lhsT=dy_codes[h][:].bitcast(E5M2_X4),
-                        lhsT_scale=dy_scales[h][:],
-                        rhs=x_codes[c][:].bitcast(E4M3_X4),
-                        rhs_scale=x_scales[c][:],
-                        start=True,
-                        stop=True,
-                    )
-                    nc.scalar.copy(out=result[:, i * BANK : (i + 1) * BANK], in_=acc[:])
-                nc.sync.dma_start(
-                    out=out[h * D : (h + 1) * D, half * STORE : (half + 1) * STORE], in_=result[:]
-                )
+                    copy(out=result[:, i * BANK : (i + 1) * BANK], in_=acc[h, half * (STORE // BANK) + i][:])
+                nc.sync.dma_start(out=out[h * D : (h + 1) * D, half * STORE : (half + 1) * STORE], in_=result[:])
 
-        regroup_x(nc.vector.tensor_copy, 0)
-        regroup_x(nc.vector.tensor_copy, 1)
+        regroup(nc.vector.tensor_copy, x_grouped[0][:], x_raw[0][:])
+        build_table()
+        regroup(nc.vector.tensor_copy, x_grouped[1][:], x_raw[1][:])
         quantise_x(0)
-        quantise_x(1)
         for h in range(QUAD):
             sum_squares(h)
-        root(0)
+        swap_pairs(0)
+        quantise_x(1)
         invert(0)
-        regroup_x(nc.scalar.copy, 2)
-        regroup_x(nc.scalar.copy, 3)
+        regroup(nc.scalar.copy, x_grouped[2][:], x_raw[2][:])
+        regroup(nc.scalar.copy, x_grouped[3][:], x_raw[3][:])
         for h in range(QUAD, NORM_LEAD):
             sum_squares(h)
 
         for k in range(HEADS + 2):
-            if k < HEADS:
-                rotate_products(k)
-            if 1 <= k <= HEADS:
-                project(k - 1)
+            rotating = k < HEADS
+            finishing = 1 <= k <= HEADS
+            if k + 1 < HEADS:
+                swap_pairs(k + 1)
+            if rotating:
+                rotate_own(k)
+            if finishing:
+                scale_dots(k - 1)
+            if rotating:
+                rotate_other(k)
+            if finishing:
+                project(k - 1, (0, 1))
+            if rotating:
+                rotate_sum(k)
+            if finishing:
+                project(k - 1, (2, 3))
                 regroup_dy(k - 1)
-            if k < HEADS:
-                rotate_sums(k)
+            if rotating:
+                dots(k)
+            if k + NORM_LEAD < HEADS:
+                sum_squares(k + NORM_LEAD)
             if k < 2:
                 quantise_x(2 + k)
             else:
                 quantise_dy(k - 2)
-            if k < HEADS:
-                project_dots(k)
-            ahead = k + NORM_LEAD
-            if ahead < HEADS:
-                sum_squares(ahead)
-                if ahead % QUAD == QUAD - 1:
-                    root(ahead // QUAD)
-                    invert(ahead // QUAD)
-            if k >= 2:
-                multiply_and_store(k - 2)
+                multiply(k - 2)
+                empty_and_store(k - 2, nc.vector.tensor_copy if k - 2 == HEADS - 1 else nc.scalar.copy)
+            if k + 1 < HEADS and (k + 1) % QUAD == 0:
+                invert((k + 1) // QUAD)

@@ -1,7 +1,6 @@
 import math
 
 import concourse.mybir as mybir
-from concourse.masks import make_identity
 
 F32 = mybir.dt.float32
 BF16 = mybir.dt.bfloat16
@@ -31,9 +30,8 @@ PAIRS_HW = DIM_HW // 2
 BANK = 512
 X_CHUNKS = C // BANK
 STORE = 2 * BANK
-QUAD = 4
-QUADS = HEADS // QUAD
-NORM_LEAD = 2 * QUAD
+GROUPS = ((0, 1), (1, 4), (4, 8), (8, 12), (12, 16))
+GROUP_OF = tuple(i for i, (first, stop) in enumerate(GROUPS) for h in range(first, stop))
 RUN = 4
 
 FLOPS = 2 * TOKENS * E * C
@@ -60,34 +58,45 @@ def tile_attention_pa_v_kernel(tc, x, w, b, norm_w, y, grad_out, out):
         nc.scalar.dma_start(out=gain[:], in_=norm_w.partition_broadcast(P))
 
         x_raw = [keep.tile([P, PACK, BANK], BF16, name="x_raw%d" % c) for c in range(X_CHUNKS)]
-        y_quad = [keep.tile([P, PACK, QUAD * D], F32, name="y_quad%d" % q) for q in range(QUADS)]
-        g_quad = [keep.tile([P, QUAD, PACK, D], BF16, name="g_quad%d" % q) for q in range(QUADS)]
+        y_group = [
+            keep.tile([P, PACK, (stop - first) * D], F32, name="y_group%d" % i) for i, (first, stop) in enumerate(GROUPS)
+        ]
+        g_group = [
+            keep.tile([P, stop - first, PACK, D], BF16, name="g_group%d" % i) for i, (first, stop) in enumerate(GROUPS)
+        ]
 
         def load_x(c):
             nc.sync.dma_start(out=x_raw[c][:], in_=x_rows[:, :, c * BANK : (c + 1) * BANK])
 
-        def load_y(q):
-            nc.sync.dma_start(out=y_quad[q][:], in_=y_rows[:, :, q * QUAD * D : (q + 1) * QUAD * D])
+        def load_y(i):
+            first, stop = GROUPS[i]
+            nc.sync.dma_start(out=y_group[i][:], in_=y_rows[:, :, first * D : stop * D])
 
-        def load_g(q):
-            nc.sync.dma_start(
-                out=g_quad[q][:].rearrange("p h j d -> p h (j d)"), in_=g_rows[:, q * QUAD : (q + 1) * QUAD, :]
-            )
+        def load_g(i):
+            first, stop = GROUPS[i]
+            nc.sync.dma_start(out=g_group[i][:].rearrange("p h j d -> p h (j d)"), in_=g_rows[:, first:stop, :])
 
-        load_x(0)
-        load_x(1)
         load_y(0)
         load_g(0)
+        load_x(0)
+        load_y(1)
+        load_g(1)
+        load_y(2)
+        load_x(1)
         load_x(2)
         load_x(3)
-        for q in range(1, QUADS):
-            load_y(q)
-            load_g(q)
+        load_g(2)
+        for i in range(3, len(GROUPS)):
+            load_y(i)
+            load_g(i)
+
+        eps = keep.tile([P, 1], F32)
+        nc.vector.memset(eps[:], EPS)
+        warm = keep.tile([P, 1], F32)
+        nc.scalar.activation(out=warm[:], in_=eps[:], func=ACT.Sin)
 
         token = keep.tile([P, PACK], I32)
         nc.gpsimd.iota(token[:], pattern=[[1, PACK]], base=0, channel_multiplier=PACK)
-        identity = keep.tile([P, P], BF16)
-        make_identity(nc, identity[:])
         grid_int = keep.tile([P, 3, PACK], I32)
         nc.vector.tensor_single_scalar(out=grid_int[:, 0, :], in_=token[:], scalar=6, op=ALU.arith_shift_right)
         nc.vector.tensor_scalar(
@@ -101,16 +110,35 @@ def tile_attention_pa_v_kernel(tc, x, w, b, norm_w, y, grad_out, out):
         nc.vector.tensor_single_scalar(out=grid_int[:, 2, :], in_=token[:], scalar=7, op=ALU.bitwise_and)
         grid = keep.tile([P, 3, PACK], F32)
         nc.vector.tensor_copy(out=grid[:], in_=grid_int[:])
-        eps = keep.tile([P, 1], F32)
-        nc.vector.memset(eps[:], EPS)
+
+        frequency = keep.tile([P, PAIRS], F32)
+        nc.vector.memset(frequency[:], 1.0)
+        frequency_hw = frequency[:, PAIRS_T:].rearrange("p (a k) -> p a k", a=2)
+        for n in (1, 2, 4, 8, 16):
+            nc.vector.tensor_scalar_mul(
+                out=frequency[:, n : min(2 * n, PAIRS_T)],
+                in0=frequency[:, 0 : min(n, PAIRS_T - n)],
+                scalar1=BASE ** (-2.0 * n / DIM_T),
+            )
+            nc.vector.tensor_scalar_mul(
+                out=frequency_hw[:, :, n : min(2 * n, PAIRS_HW)],
+                in0=frequency_hw[:, :, 0 : min(n, PAIRS_HW - n)],
+                scalar1=BASE ** (-2.0 * n / DIM_HW),
+            )
 
         turn = keep.tile([P, 2, PACK, PAIRS], F32)
-        for k in range(PAIRS_T):
-            nc.vector.tensor_scalar_mul(out=turn[:, 1, :, k], in0=grid[:, 0, :], scalar1=BASE ** (-2.0 * k / DIM_T))
-        turn_hw = turn[:, 1, :, PAIRS_T:].rearrange("p j (a k) -> p j a k", a=2)
-        grid_hw = grid[:, 1:3, :].rearrange("p a j -> p j a")
-        for k in range(PAIRS_HW):
-            nc.vector.tensor_scalar_mul(out=turn_hw[:, :, :, k], in0=grid_hw, scalar1=BASE ** (-2.0 * k / DIM_HW))
+        nc.vector.tensor_tensor(
+            out=turn[:, 1, :, :PAIRS_T],
+            in0=frequency[:, :PAIRS_T].unsqueeze(1).to_broadcast([P, PACK, PAIRS_T]),
+            in1=grid[:, 0, :].unsqueeze(2).to_broadcast([P, PACK, PAIRS_T]),
+            op=ALU.mult,
+        )
+        nc.vector.tensor_tensor(
+            out=turn[:, 1, :, PAIRS_T:].rearrange("p j (a k) -> p j a k", a=2),
+            in0=frequency_hw.unsqueeze(1).to_broadcast([P, PACK, 2, PAIRS_HW]),
+            in1=grid[:, 1:3, :].rearrange("p a j -> p j a").unsqueeze(3).to_broadcast([P, PACK, 2, PAIRS_HW]),
+            op=ALU.mult,
+        )
         nc.vector.tensor_scalar_add(out=turn[:, 0], in0=turn[:, 1], scalar1=0.5 * math.pi)
         full_turn = keep.tile([P, 2, PACK, PAIRS], F32)
         nc.vector.tensor_scalar(
@@ -119,13 +147,15 @@ def tile_attention_pa_v_kernel(tc, x, w, b, norm_w, y, grad_out, out):
         wrapped = keep.tile([P, 2, PACK, PAIRS], F32)
         nc.vector.tensor_sub(out=wrapped[:], in0=turn[:], in1=full_turn[:])
         cos_sin = keep.tile([P, 2, PACK, PAIRS], F32)
-        nc.scalar.activation(out=cos_sin[:], in_=wrapped[:], func=ACT.Sin)
+
+        def sines():
+            nc.scalar.activation(out=cos_sin[:], in_=wrapped[:], func=ACT.Sin)
 
         gains = keep.tile([P, 2, PAIRS, 2], F32)
         gain_pairs = gain[:].rearrange("p (m e) -> p m e", e=2)
         nc.vector.tensor_copy(out=gains[:, 0], in_=gain_pairs)
-        nc.vector.tensor_copy(out=gains[:, 1, :, 0], in_=gain_pairs[:, :, 0])
-        nc.vector.tensor_scalar_mul(out=gains[:, 1, :, 1], in0=gain_pairs[:, :, 1], scalar1=-1.0)
+        nc.vector.tensor_copy(out=gains[:, 1, :, 1], in_=gain_pairs[:, :, 0])
+        nc.vector.tensor_scalar_mul(out=gains[:, 1, :, 0], in0=gain_pairs[:, :, 1], scalar1=-1.0)
         table = keep.tile([P, 2, PACK, D], F32)
 
         def build_table():
@@ -140,6 +170,9 @@ def tile_attention_pa_v_kernel(tc, x, w, b, norm_w, y, grad_out, out):
         x_codes = [keep.tile([P, BANK], U32, name="x_codes%d" % c, align_bytes=64) for c in range(X_CHUNKS)]
         x_scales = [keep.tile([P, BANK], U8, name="x_scales%d" % c, align_bytes=64) for c in range(X_CHUNKS)]
 
+        def regroup_x(copy, c):
+            regroup(copy, x_grouped[c][:], x_raw[c][:])
+
         def quantise_x(c):
             nc.vector.quantize_mx(
                 out=x_codes[c][:].bitcast(E4M3_X4),
@@ -147,86 +180,60 @@ def tile_attention_pa_v_kernel(tc, x, w, b, norm_w, y, grad_out, out):
                 in_=x_grouped[c][:].rearrange("p c j -> p (c j)"),
             )
 
-        square_sum = [keep.tile([P, QUAD, PACK], F32, name="square_sum%d" % q) for q in range(QUADS)]
-        rms = [keep.tile([P, QUAD, PACK], F32, name="rms%d" % q) for q in range(QUADS)]
-        r = [keep.tile([P, QUAD, PACK], F32, name="r%d" % q) for q in range(QUADS)]
-        r_squared = [keep.tile([P, QUAD, PACK], F32, name="r_squared%d" % q) for q in range(QUADS)]
+        square_sum = keep.tile([P, HEADS, PACK], F32)
+        rms = keep.tile([P, HEADS, PACK], F32)
+        r = keep.tile([P, HEADS, PACK], F32)
+        r_squared = keep.tile([P, HEADS, PACK], F32)
 
         def y_of(h, j):
-            return y_quad[h // QUAD][:, j, (h % QUAD) * D : (h % QUAD + 1) * D]
+            i = GROUP_OF[h]
+            at = (h - GROUPS[i][0]) * D
+            return y_group[i][:, j, at : at + D]
 
-        def r_of(h, j):
-            return r[h // QUAD][:, h % QUAD, j : j + 1]
+        def g_of(h, j):
+            i = GROUP_OF[h]
+            return g_group[i][:, h - GROUPS[i][0], j, :]
 
         def sum_squares(h):
             squares = work.tile([P, PACK, D], F32)
             for j in range(PACK):
                 nc.scalar.activation(
-                    out=squares[:, j, :],
-                    in_=y_of(h, j),
-                    func=ACT.Square,
-                    accum_out=square_sum[h // QUAD][:, h % QUAD, j : j + 1],
-                )
-            if h % QUAD == QUAD - 1:
-                q = h // QUAD
-                nc.scalar.activation(
-                    out=rms[q][:], in_=square_sum[q][:], func=ACT.Sqrt, scale=1.0 / D, bias=eps[:, 0:1]
+                    out=squares[:, j, :], in_=y_of(h, j), func=ACT.Square, accum_out=square_sum[:, h, j : j + 1]
                 )
 
-        def invert(q):
-            nc.vector.reciprocal(out=r[q][:], in_=rms[q][:])
-            nc.vector.tensor_mul(out=r_squared[q][:], in0=r[q][:], in1=r[q][:])
+        def root(i):
+            first, stop = GROUPS[i]
+            nc.scalar.activation(
+                out=rms[:, first:stop, :], in_=square_sum[:, first:stop, :], func=ACT.Sqrt, scale=1.0 / D, bias=eps[:, 0:1]
+            )
 
-        swapped, own, other, dn, dot, coefficient, dy_rows, dy_grouped, dy_codes, dy_scales, acc = (
-            {},
-            {},
-            {},
-            {},
-            {},
-            {},
-            {},
-            {},
-            {},
-            {},
-            {},
-        )
+        def invert(i):
+            first, stop = GROUPS[i]
+            nc.vector.reciprocal(out=r[:, first:stop, :], in_=rms[:, first:stop, :])
+            nc.vector.tensor_mul(out=r_squared[:, first:stop, :], in0=r[:, first:stop, :], in1=r[:, first:stop, :])
 
-        def swap_pairs(h):
-            bank = psum.tile([P, PACK, PAIRS, 2], F32, name="swapped")
-            pairs = g_quad[h // QUAD][:, h % QUAD].rearrange("p j (m e) -> p j m e", e=2)
-            for e in range(2):
-                nc.tensor.matmul(
-                    out=bank[:, :, :, e], lhsT=identity[:], rhs=pairs[:, :, :, 1 - e], start=True, stop=True
-                )
-            swapped[h] = bank
+        products, dn, dot, coefficient, scaled_y, dy_grouped, dy_codes, dy_scales, acc = {}, {}, {}, {}, {}, {}, {}, {}, {}
 
-        def rotate_own(h):
-            own[h] = work.tile([P, PACK, D], F32, name="own")
+        def rotate_products(h):
+            products[h] = work.tile([P, 2, PACK, D], F32, name="products")
             for j in range(PACK):
                 nc.vector.scalar_tensor_tensor(
-                    out=own[h][:, j, :],
-                    in0=g_quad[h // QUAD][:, h % QUAD, j, :],
-                    scalar=r_of(h, j),
-                    in1=table[:, 0, j, :],
-                    op0=ALU.mult,
-                    op1=ALU.mult,
-                )
-
-        def rotate_other(h):
-            other[h] = work.tile([P, PACK, D], F32, name="other")
-            for j in range(PACK):
-                nc.vector.scalar_tensor_tensor(
-                    out=other[h][:, j, :],
-                    in0=swapped[h][:, j].rearrange("p m e -> p (m e)"),
-                    scalar=r_of(h, j),
-                    in1=table[:, 1, j, :],
+                    out=products[h][:, :, j, :],
+                    in0=g_of(h, j).unsqueeze(1).to_broadcast([P, 2, D]),
+                    scalar=r[:, h, j : j + 1],
+                    in1=table[:, :, j, :],
                     op0=ALU.mult,
                     op1=ALU.mult,
                 )
 
         def rotate_sum(h):
-            dn[h] = work.tile([P, PACK, D], F32, name="dn")
-            nc.vector.tensor_add(out=dn[h][:], in0=own[h][:], in1=other[h][:])
+            dn[h] = work.tile([P, PACK, D], F32, name="dn", bufs=4)
+            nc.vector.tensor_tensor(
+                out=dn[h][:].rearrange("p j (m e) -> p (j m) e", e=2),
+                in0=products[h][:, 0].rearrange("p j (m e) -> p (j m) e", e=2),
+                in1=products[h][:, 1].rearrange("p j (m e) -> p (j m) e", e=2)[:, :, ::-1],
+                op=ALU.add,
+            )
 
         def dots(h):
             dot[h] = work.tile([P, PACK], F32, name="dot")
@@ -248,27 +255,26 @@ def tile_attention_pa_v_kernel(tc, x, w, b, norm_w, y, grad_out, out):
                 out=coefficient[h][:],
                 in0=dot[h][:],
                 scalar=-1.0 / D,
-                in1=r_squared[h // QUAD][:, h % QUAD, :],
+                in1=r_squared[:, h, :],
                 op0=ALU.mult,
                 op1=ALU.mult,
             )
 
-        def project(h, tokens):
-            if h not in dy_rows:
-                dy_rows[h] = work.tile([P, PACK, D], BF16, name="dy_rows")
-            for j in tokens:
-                nc.vector.scalar_tensor_tensor(
-                    out=dy_rows[h][:, j, :],
-                    in0=y_of(h, j),
-                    scalar=coefficient[h][:, j : j + 1],
-                    in1=dn[h][:, j, :],
-                    op0=ALU.mult,
-                    op1=ALU.add,
+        def scale_y(h):
+            scaled_y[h] = work.tile([P, PACK, D], F32, name="scaled_y")
+            for j in range(PACK):
+                nc.scalar.activation(
+                    out=scaled_y[h][:, j, :], in_=y_of(h, j), func=ACT.Copy, scale=coefficient[h][:, j : j + 1]
                 )
 
-        def regroup_dy(h):
+        def project(h):
             dy_grouped[h] = work.tile([P, D, PACK], BF16, name="dy_grouped", align_bytes=64)
-            regroup(nc.scalar.copy, dy_grouped[h][:], dy_rows[h][:])
+            nc.vector.tensor_tensor(
+                out=dy_grouped[h][:].rearrange("p (c i) j -> p c j i", i=RUN),
+                in0=dn[h][:].rearrange("p j (c i) -> p c j i", i=RUN),
+                in1=scaled_y[h][:].rearrange("p j (c i) -> p c j i", i=RUN),
+                op=ALU.add,
+            )
 
         def quantise_dy(h):
             dy_codes[h] = work.tile([P, D], U32, name="dy_codes", align_bytes=64)
@@ -281,7 +287,7 @@ def tile_attention_pa_v_kernel(tc, x, w, b, norm_w, y, grad_out, out):
 
         def multiply(h):
             for c in range(X_CHUNKS):
-                acc[h, c] = psum.tile([P, BANK], F32, name="acc", bufs=6)
+                acc[h, c] = psum.tile([P, BANK], F32, name="acc", bufs=8)
                 nc.tensor.matmul_mx(
                     out=acc[h, c][:],
                     lhsT=dy_codes[h][:].bitcast(E5M2_X4),
@@ -292,54 +298,64 @@ def tile_attention_pa_v_kernel(tc, x, w, b, norm_w, y, grad_out, out):
                     stop=True,
                 )
 
-        def empty_and_store(h, copy):
+        def empty_and_store(h, copies):
             for half in range(C // STORE):
                 result = work.tile([P, STORE], F32, name="result", bufs=4)
                 for i in range(STORE // BANK):
-                    copy(out=result[:, i * BANK : (i + 1) * BANK], in_=acc[h, half * (STORE // BANK) + i][:])
+                    c = half * (STORE // BANK) + i
+                    copies[c](out=result[:, i * BANK : (i + 1) * BANK], in_=acc[h, c][:])
                 nc.sync.dma_start(out=out[h * D : (h + 1) * D, half * STORE : (half + 1) * STORE], in_=result[:])
 
-        regroup(nc.vector.tensor_copy, x_grouped[0][:], x_raw[0][:])
+        sum_squares(0)
+        sines()
+        root(0)
+        regroup_x(nc.vector.tensor_copy, 0)
         build_table()
-        regroup(nc.vector.tensor_copy, x_grouped[1][:], x_raw[1][:])
-        quantise_x(0)
-        for h in range(QUAD):
-            sum_squares(h)
-        swap_pairs(0)
-        quantise_x(1)
         invert(0)
-        regroup(nc.scalar.copy, x_grouped[2][:], x_raw[2][:])
-        regroup(nc.scalar.copy, x_grouped[3][:], x_raw[3][:])
-        for h in range(QUAD, NORM_LEAD):
+        for h in range(1, 4):
             sum_squares(h)
+        root(1)
+        for h in range(4, 8):
+            sum_squares(h)
+        root(2)
+        regroup_x(nc.scalar.copy, 2)
 
+        scalar_only = (nc.scalar.copy,) * X_CHUNKS
+        both = (nc.scalar.copy, nc.vector.tensor_copy) * (X_CHUNKS // 2)
         for k in range(HEADS + 2):
             rotating = k < HEADS
-            finishing = 1 <= k <= HEADS
-            if k + 1 < HEADS:
-                swap_pairs(k + 1)
             if rotating:
-                rotate_own(k)
-            if finishing:
+                rotate_products(k)
+            if 1 <= k <= HEADS:
                 scale_dots(k - 1)
-            if rotating:
-                rotate_other(k)
-            if finishing:
-                project(k - 1, (0, 1))
+                scale_y(k - 1)
+            if k >= 2:
+                project(k - 2)
+            if k == 0:
+                quantise_x(0)
+            if k == 1:
+                quantise_x(1)
             if rotating:
                 rotate_sum(k)
-            if finishing:
-                project(k - 1, (2, 3))
-                regroup_dy(k - 1)
-            if rotating:
-                dots(k)
-            if k + NORM_LEAD < HEADS:
-                sum_squares(k + NORM_LEAD)
-            if k < 2:
-                quantise_x(2 + k)
-            else:
+            if k + 8 < HEADS:
+                sum_squares(k + 8)
+            if k in (3, 7):
+                root(k // 4 + 3)
+            if k == 0:
+                regroup_x(nc.vector.tensor_copy, 1)
+            if k == 1:
+                regroup_x(nc.vector.tensor_copy, 3)
+            if k == 2:
+                quantise_x(3)
+            if k >= 2:
                 quantise_dy(k - 2)
                 multiply(k - 2)
-                empty_and_store(k - 2, nc.vector.tensor_copy if k - 2 == HEADS - 1 else nc.scalar.copy)
-            if k + 1 < HEADS and (k + 1) % QUAD == 0:
-                invert((k + 1) // QUAD)
+                empty_and_store(k - 2, both if k - 2 == HEADS - 1 else scalar_only)
+            if rotating:
+                dots(k)
+            if k == 1:
+                quantise_x(2)
+            if k == 0:
+                invert(1)
+            if k in (1, 5, 9):
+                invert(k // 4 + 2)

@@ -54,8 +54,11 @@ def tile_attention_pa_v_kernel(tc, x, w, b, norm_w, y, grad_out, out):
     with tc.tile_pool(name="keep", bufs=1) as keep, tc.tile_pool(name="work", bufs=3) as work, tc.psum_pool(
         name="psum", bufs=2
     ) as psum, tc.manual_schedule():
-        gain = keep.tile([P, D], BF16)
-        nc.scalar.dma_start(out=gain[:], in_=norm_w.partition_broadcast(P))
+        gain_row = keep.tile([P, D], BF16)
+        nc.gpsimd.memset(gain_row[:], 0.0)
+        ones = keep.tile([P, P], BF16)
+        nc.gpsimd.memset(ones[:], 1.0)
+        nc.scalar.dma_start(out=gain_row[0:1, :], in_=norm_w.unsqueeze(0))
 
         x_raw = [keep.tile([P, PACK, BANK], BF16, name="x_raw%d" % c) for c in range(X_CHUNKS)]
         y_group = [
@@ -152,6 +155,8 @@ def tile_attention_pa_v_kernel(tc, x, w, b, norm_w, y, grad_out, out):
             nc.scalar.activation(out=cos_sin[:], in_=wrapped[:], func=ACT.Sin)
 
         gains = keep.tile([P, 2, PAIRS, 2], F32)
+        gain = psum.tile([P, D], F32, name="acc", bufs=8)
+        nc.tensor.matmul(out=gain[:], lhsT=ones[:], rhs=gain_row[:], start=True, stop=True)
         gain_pairs = gain[:].rearrange("p (m e) -> p m e", e=2)
         nc.vector.tensor_copy(out=gains[:, 0], in_=gain_pairs)
         nc.vector.tensor_copy(out=gains[:, 1, :, 1], in_=gain_pairs[:, :, 0])
@@ -183,7 +188,7 @@ def tile_attention_pa_v_kernel(tc, x, w, b, norm_w, y, grad_out, out):
         square_sum = keep.tile([P, HEADS, PACK], F32)
         rms = keep.tile([P, HEADS, PACK], F32)
         r = keep.tile([P, HEADS, PACK], F32)
-        r_squared = keep.tile([P, HEADS, PACK], F32)
+        pull = keep.tile([P, HEADS, PACK], F32)
 
         def y_of(h, j):
             i = GROUP_OF[h]
@@ -210,9 +215,16 @@ def tile_attention_pa_v_kernel(tc, x, w, b, norm_w, y, grad_out, out):
         def invert(i):
             first, stop = GROUPS[i]
             nc.vector.reciprocal(out=r[:, first:stop, :], in_=rms[:, first:stop, :])
-            nc.vector.tensor_mul(out=r_squared[:, first:stop, :], in0=r[:, first:stop, :], in1=r[:, first:stop, :])
+            nc.vector.scalar_tensor_tensor(
+                out=pull[:, first:stop, :],
+                in0=r[:, first:stop, :],
+                scalar=-1.0 / D,
+                in1=r[:, first:stop, :],
+                op0=ALU.mult,
+                op1=ALU.mult,
+            )
 
-        products, dn, dot, coefficient, scaled_y, dy_grouped, dy_codes, dy_scales, acc = {}, {}, {}, {}, {}, {}, {}, {}, {}
+        products, dn, coefficient, scaled_y, dy_grouped, dy_codes, dy_scales, acc = {}, {}, {}, {}, {}, {}, {}, {}
 
         def rotate_products(h):
             products[h] = work.tile([P, 2, PACK, D], F32, name="products")
@@ -236,36 +248,30 @@ def tile_attention_pa_v_kernel(tc, x, w, b, norm_w, y, grad_out, out):
             )
 
         def dots(h):
-            dot[h] = work.tile([P, PACK], F32, name="dot")
+            coefficient[h] = work.tile([P, PACK], F32, name="coefficient")
             terms = work.tile([P, PACK, D], F32, name="terms")
             for j in range(PACK):
                 nc.vector.scalar_tensor_tensor(
                     out=terms[:, j, :],
                     in0=dn[h][:, j, :],
-                    scalar=1.0,
+                    scalar=pull[:, h, j : j + 1],
                     in1=y_of(h, j),
                     op0=ALU.mult,
                     op1=ALU.mult,
-                    accum_out=dot[h][:, j : j + 1],
+                    accum_out=coefficient[h][:, j : j + 1],
                 )
 
-        def scale_dots(h):
-            coefficient[h] = work.tile([P, PACK], F32, name="coefficient")
-            nc.vector.scalar_tensor_tensor(
-                out=coefficient[h][:],
-                in0=dot[h][:],
-                scalar=-1.0 / D,
-                in1=r_squared[:, h, :],
-                op0=ALU.mult,
-                op1=ALU.mult,
-            )
-
-        def scale_y(h):
+        def scale_y(h, on_vector=False):
             scaled_y[h] = work.tile([P, PACK, D], F32, name="scaled_y")
             for j in range(PACK):
-                nc.scalar.activation(
-                    out=scaled_y[h][:, j, :], in_=y_of(h, j), func=ACT.Copy, scale=coefficient[h][:, j : j + 1]
-                )
+                if on_vector:
+                    nc.vector.tensor_scalar_mul(
+                        out=scaled_y[h][:, j, :], in0=y_of(h, j), scalar1=coefficient[h][:, j : j + 1]
+                    )
+                else:
+                    nc.scalar.activation(
+                        out=scaled_y[h][:, j, :], in_=y_of(h, j), func=ACT.Copy, scale=coefficient[h][:, j : j + 1]
+                    )
 
         def project(h):
             dy_grouped[h] = work.tile([P, D, PACK], BF16, name="dy_grouped", align_bytes=64)
@@ -298,13 +304,19 @@ def tile_attention_pa_v_kernel(tc, x, w, b, norm_w, y, grad_out, out):
                     stop=True,
                 )
 
-        def empty_and_store(h, copies):
-            for half in range(C // STORE):
-                result = work.tile([P, STORE], F32, name="result", bufs=4)
-                for i in range(STORE // BANK):
-                    c = half * (STORE // BANK) + i
-                    copies[c](out=result[:, i * BANK : (i + 1) * BANK], in_=acc[h, c][:])
-                nc.sync.dma_start(out=out[h * D : (h + 1) * D, half * STORE : (half + 1) * STORE], in_=result[:])
+        result = {}
+
+        def empty(h, c, copy, store_each=False):
+            half, i = divmod(c, STORE // BANK)
+            if i == 0:
+                result[h, half] = work.tile([P, STORE], F32, name="result", bufs=6)
+            copy(out=result[h, half][:, i * BANK : (i + 1) * BANK], in_=acc[h, c][:])
+            if store_each:
+                nc.sync.dma_start(
+                    out=out[h * D : (h + 1) * D, c * BANK : (c + 1) * BANK], in_=result[h, half][:, i * BANK : (i + 1) * BANK]
+                )
+            elif i == STORE // BANK - 1:
+                nc.sync.dma_start(out=out[h * D : (h + 1) * D, half * STORE : (half + 1) * STORE], in_=result[h, half][:])
 
         sum_squares(0)
         sines()
@@ -320,23 +332,15 @@ def tile_attention_pa_v_kernel(tc, x, w, b, norm_w, y, grad_out, out):
         root(2)
         regroup_x(nc.scalar.copy, 2)
 
-        scalar_only = (nc.scalar.copy,) * X_CHUNKS
-        both = (nc.scalar.copy, nc.vector.tensor_copy) * (X_CHUNKS // 2)
-        for k in range(HEADS + 2):
-            rotating = k < HEADS
-            if rotating:
-                rotate_products(k)
-            if 1 <= k <= HEADS:
-                scale_dots(k - 1)
+        for k in range(HEADS):
+            rotate_products(k)
+            if k >= 1:
                 scale_y(k - 1)
             if k >= 2:
                 project(k - 2)
-            if k == 0:
-                quantise_x(0)
-            if k == 1:
-                quantise_x(1)
-            if rotating:
-                rotate_sum(k)
+            if k < 2:
+                quantise_x(k)
+            rotate_sum(k)
             if k + 8 < HEADS:
                 sum_squares(k + 8)
             if k in (3, 7):
@@ -350,12 +354,26 @@ def tile_attention_pa_v_kernel(tc, x, w, b, norm_w, y, grad_out, out):
             if k >= 2:
                 quantise_dy(k - 2)
                 multiply(k - 2)
-                empty_and_store(k - 2, both if k - 2 == HEADS - 1 else scalar_only)
-            if rotating:
-                dots(k)
+                for c in range(X_CHUNKS):
+                    empty(k - 2, c, nc.scalar.copy)
+            dots(k)
             if k == 1:
                 quantise_x(2)
             if k == 0:
                 invert(1)
             if k in (1, 5, 9):
                 invert(k // 4 + 2)
+
+        project(HEADS - 2)
+        scale_y(HEADS - 1, on_vector=True)
+        quantise_dy(HEADS - 2)
+        multiply(HEADS - 2)
+        project(HEADS - 1)
+        empty(HEADS - 2, 0, nc.scalar.copy)
+        empty(HEADS - 2, 1, nc.scalar.copy)
+        quantise_dy(HEADS - 1)
+        multiply(HEADS - 1)
+        empty(HEADS - 2, 2, nc.vector.tensor_copy)
+        empty(HEADS - 2, 3, nc.vector.tensor_copy)
+        for c in range(X_CHUNKS):
+            empty(HEADS - 1, c, nc.vector.tensor_copy if c % 2 == 1 else nc.scalar.copy, store_each=True)

@@ -54,11 +54,10 @@ def tile_attention_pa_v_kernel(tc, x, w, b, norm_w, y, grad_out, out):
     with tc.tile_pool(name="keep", bufs=1) as keep, tc.tile_pool(name="work", bufs=3) as work, tc.psum_pool(
         name="psum", bufs=2
     ) as psum, tc.manual_schedule():
+        gain_landing = keep.tile([1, D], BF16)
+        nc.scalar.dma_start(out=gain_landing[:], in_=norm_w.unsqueeze(0))
         gain_row = keep.tile([P, D], BF16)
-        nc.gpsimd.memset(gain_row[:], 0.0)
-        ones = keep.tile([P, P], BF16)
-        nc.gpsimd.memset(ones[:], 1.0)
-        nc.scalar.dma_start(out=gain_row[0:1, :], in_=norm_w.unsqueeze(0))
+        nc.vector.memset(gain_row[:], 0.0)
 
         x_raw = [keep.tile([P, PACK, BANK], BF16, name="x_raw%d" % c) for c in range(X_CHUNKS)]
         y_group = [
@@ -86,12 +85,13 @@ def tile_attention_pa_v_kernel(tc, x, w, b, norm_w, y, grad_out, out):
         load_g(1)
         load_y(2)
         load_x(1)
-        load_x(2)
+        load_y(3)
         load_x(3)
+        load_x(2)
         load_g(2)
-        for i in range(3, len(GROUPS)):
-            load_y(i)
-            load_g(i)
+        load_y(4)
+        load_g(3)
+        load_g(4)
 
         eps = keep.tile([P, 1], F32)
         nc.vector.memset(eps[:], EPS)
@@ -100,24 +100,25 @@ def tile_attention_pa_v_kernel(tc, x, w, b, norm_w, y, grad_out, out):
 
         token = keep.tile([P, PACK], I32)
         nc.gpsimd.iota(token[:], pattern=[[1, PACK]], base=0, channel_multiplier=PACK)
+        ones = keep.tile([P, P], BF16)
+        nc.gpsimd.memset(ones[:], 1.0)
         grid_int = keep.tile([P, 3, PACK], I32)
-        nc.vector.tensor_single_scalar(out=grid_int[:, 0, :], in_=token[:], scalar=6, op=ALU.arith_shift_right)
-        nc.vector.tensor_scalar(
-            out=grid_int[:, 1, :],
-            in0=token[:],
-            scalar1=3,
-            scalar2=7,
-            op0=ALU.arith_shift_right,
-            op1=ALU.bitwise_and,
-        )
-        nc.vector.tensor_single_scalar(out=grid_int[:, 2, :], in_=token[:], scalar=7, op=ALU.bitwise_and)
         grid = keep.tile([P, 3, PACK], F32)
-        nc.vector.tensor_copy(out=grid[:], in_=grid_int[:])
+
+        def coordinate(a):
+            nc.vector.tensor_scalar(
+                out=grid_int[:, a, :],
+                in0=token[:],
+                scalar1=6 - 3 * a,
+                scalar2=7,
+                op0=ALU.arith_shift_right,
+                op1=ALU.bitwise_and,
+            )
 
         frequency = keep.tile([P, PAIRS], F32)
         nc.vector.memset(frequency[:], 1.0)
         frequency_hw = frequency[:, PAIRS_T:].rearrange("p (a k) -> p a k", a=2)
-        for n in (1, 2, 4, 8, 16):
+        for level, n in enumerate((1, 2, 4, 8, 16)):
             nc.vector.tensor_scalar_mul(
                 out=frequency[:, n : min(2 * n, PAIRS_T)],
                 in0=frequency[:, 0 : min(n, PAIRS_T - n)],
@@ -128,6 +129,9 @@ def tile_attention_pa_v_kernel(tc, x, w, b, norm_w, y, grad_out, out):
                 in0=frequency_hw[:, :, 0 : min(n, PAIRS_HW - n)],
                 scalar1=BASE ** (-2.0 * n / DIM_HW),
             )
+            if 1 <= level <= 3:
+                coordinate(level - 1)
+        nc.vector.tensor_copy(out=grid[:], in_=grid_int[:])
 
         turn = keep.tile([P, 2, PACK, PAIRS], F32)
         nc.vector.tensor_tensor(
@@ -156,14 +160,15 @@ def tile_attention_pa_v_kernel(tc, x, w, b, norm_w, y, grad_out, out):
 
         gains = keep.tile([P, 2, PAIRS, 2], F32)
         gain = psum.tile([P, D], F32, name="acc", bufs=8)
+        nc.vector.tensor_copy(out=gain_row[0:1, :], in_=gain_landing[:])
         nc.tensor.matmul(out=gain[:], lhsT=ones[:], rhs=gain_row[:], start=True, stop=True)
         gain_pairs = gain[:].rearrange("p (m e) -> p m e", e=2)
-        nc.vector.tensor_copy(out=gains[:, 0], in_=gain_pairs)
-        nc.vector.tensor_copy(out=gains[:, 1, :, 1], in_=gain_pairs[:, :, 0])
-        nc.vector.tensor_scalar_mul(out=gains[:, 1, :, 0], in0=gain_pairs[:, :, 1], scalar1=-1.0)
         table = keep.tile([P, 2, PACK, D], F32)
 
         def build_table():
+            nc.vector.tensor_copy(out=gains[:, 0], in_=gain_pairs)
+            nc.vector.tensor_copy(out=gains[:, 1, :, 1], in_=gain_pairs[:, :, 0])
+            nc.vector.tensor_scalar_mul(out=gains[:, 1, :, 0], in0=gain_pairs[:, :, 1], scalar1=-1.0)
             nc.vector.tensor_tensor(
                 out=table[:].rearrange("p k j (m e) -> p k j m e", e=2),
                 in0=cos_sin[:].unsqueeze(4).to_broadcast([P, 2, PACK, PAIRS, 2]),
@@ -330,7 +335,6 @@ def tile_attention_pa_v_kernel(tc, x, w, b, norm_w, y, grad_out, out):
         for h in range(4, 8):
             sum_squares(h)
         root(2)
-        regroup_x(nc.scalar.copy, 2)
 
         for k in range(HEADS):
             rotate_products(k)
@@ -341,16 +345,20 @@ def tile_attention_pa_v_kernel(tc, x, w, b, norm_w, y, grad_out, out):
             if k < 2:
                 quantise_x(k)
             rotate_sum(k)
-            if k + 8 < HEADS:
-                sum_squares(k + 8)
-            if k in (3, 7):
+            if k < 2:
+                sum_squares(8 + 2 * k)
+                sum_squares(9 + 2 * k)
+            elif k + 10 < HEADS:
+                sum_squares(k + 10)
+            if k in (1, 5):
                 root(k // 4 + 3)
             if k == 0:
                 regroup_x(nc.vector.tensor_copy, 1)
             if k == 1:
                 regroup_x(nc.vector.tensor_copy, 3)
+                regroup_x(nc.scalar.copy, 2)
             if k == 2:
-                quantise_x(3)
+                quantise_x(2)
             if k >= 2:
                 quantise_dy(k - 2)
                 multiply(k - 2)
@@ -358,7 +366,7 @@ def tile_attention_pa_v_kernel(tc, x, w, b, norm_w, y, grad_out, out):
                     empty(k - 2, c, nc.scalar.copy)
             dots(k)
             if k == 1:
-                quantise_x(2)
+                quantise_x(3)
             if k == 0:
                 invert(1)
             if k in (1, 5, 9):

@@ -29,7 +29,6 @@ PAIRS_HW = DIM_HW // 2
 
 BANK = 512
 X_CHUNKS = C // BANK
-STORE = 2 * BANK
 GROUPS = ((0, 1), (1, 4), (4, 8), (8, 12), (12, 16))
 GROUP_OF = tuple(i for i, (first, stop) in enumerate(GROUPS) for h in range(first, stop))
 RUN = 4
@@ -309,19 +308,10 @@ def tile_attention_pa_v_kernel(tc, x, w, b, norm_w, y, grad_out, out):
                     stop=True,
                 )
 
-        result = {}
-
-        def empty(h, c, copy, store_each=False):
-            half, i = divmod(c, STORE // BANK)
-            if i == 0:
-                result[h, half] = work.tile([P, STORE], F32, name="result", bufs=6)
-            copy(out=result[h, half][:, i * BANK : (i + 1) * BANK], in_=acc[h, c][:])
-            if store_each:
-                nc.sync.dma_start(
-                    out=out[h * D : (h + 1) * D, c * BANK : (c + 1) * BANK], in_=result[h, half][:, i * BANK : (i + 1) * BANK]
-                )
-            elif i == STORE // BANK - 1:
-                nc.sync.dma_start(out=out[h * D : (h + 1) * D, half * STORE : (half + 1) * STORE], in_=result[h, half][:])
+        def empty(h, c, copy):
+            result = work.tile([P, BANK], F32, name="result", bufs=8)
+            copy(out=result[:], in_=acc[h, c][:])
+            nc.sync.dma_start(out=out[h * D : (h + 1) * D, c * BANK : (c + 1) * BANK], in_=result[:])
 
         sum_squares(0)
         sines()
@@ -384,4 +374,4 @@ def tile_attention_pa_v_kernel(tc, x, w, b, norm_w, y, grad_out, out):
         empty(HEADS - 2, 2, nc.vector.tensor_copy)
         empty(HEADS - 2, 3, nc.vector.tensor_copy)
         for c in range(X_CHUNKS):
-            empty(HEADS - 1, c, nc.vector.tensor_copy if c % 2 == 1 else nc.scalar.copy, store_each=True)
+            empty(HEADS - 1, c, nc.vector.tensor_copy if c % 2 == 1 else nc.scalar.copy)

@@ -164,10 +164,12 @@ def tile_attention_pa_v_kernel(tc, x, w, b, norm_w, y, grad_out, out):
         gain_pairs = gain[:].rearrange("p (m e) -> p m e", e=2)
         table = keep.tile([P, 2, PACK, D], F32)
 
-        def build_table():
+        def sort_gains():
             nc.vector.tensor_copy(out=gains[:, 0], in_=gain_pairs)
             nc.vector.tensor_copy(out=gains[:, 1, :, 1], in_=gain_pairs[:, :, 0])
             nc.vector.tensor_scalar_mul(out=gains[:, 1, :, 0], in0=gain_pairs[:, :, 1], scalar1=-1.0)
+
+        def build_table():
             nc.vector.tensor_tensor(
                 out=table[:].rearrange("p k j (m e) -> p k j m e", e=2),
                 in0=cos_sin[:].unsqueeze(4).to_broadcast([P, 2, PACK, PAIRS, 2]),
@@ -230,9 +232,10 @@ def tile_attention_pa_v_kernel(tc, x, w, b, norm_w, y, grad_out, out):
 
         products, dn, coefficient, scaled_y, dy_grouped, dy_codes, dy_scales, acc = {}, {}, {}, {}, {}, {}, {}, {}
 
-        def rotate_products(h):
-            products[h] = work.tile([P, 2, PACK, D], F32, name="products")
-            for j in range(PACK):
+        def rotate_products(h, tokens):
+            if h not in products:
+                products[h] = work.tile([P, 2, PACK, D], F32, name="products")
+            for j in tokens:
                 nc.vector.scalar_tensor_tensor(
                     out=products[h][:, :, j, :],
                     in0=g_of(h, j).unsqueeze(1).to_broadcast([P, 2, D]),
@@ -317,6 +320,8 @@ def tile_attention_pa_v_kernel(tc, x, w, b, norm_w, y, grad_out, out):
         sines()
         root(0)
         regroup_x(nc.vector.tensor_copy, 0)
+        sort_gains()
+        quantise_x(0)
         build_table()
         invert(0)
         for h in range(1, 4):
@@ -326,24 +331,26 @@ def tile_attention_pa_v_kernel(tc, x, w, b, norm_w, y, grad_out, out):
             sum_squares(h)
         root(2)
 
+        rotate_products(0, (0, 1))
         for k in range(HEADS):
-            rotate_products(k)
+            rotate_products(k, (2, 3))
             if k >= 1:
                 scale_y(k - 1)
             if k >= 2:
                 project(k - 2)
-            if k < 2:
-                quantise_x(k)
+            if k == 1:
+                quantise_x(1)
             rotate_sum(k)
             if k < 2:
                 sum_squares(8 + 2 * k)
                 sum_squares(9 + 2 * k)
-            elif k + 10 < HEADS:
-                sum_squares(k + 10)
-            if k in (1, 5):
-                root(k // 4 + 3)
+            elif k % 2 == 0 and k // 2 + 11 < HEADS:
+                sum_squares(k // 2 + 11)
+            if k in (1, 8):
+                root(k // 8 + 3)
             if k == 0:
                 regroup_x(nc.vector.tensor_copy, 1)
+                invert(1)
             if k == 1:
                 regroup_x(nc.vector.tensor_copy, 3)
                 regroup_x(nc.scalar.copy, 2)
@@ -354,11 +361,11 @@ def tile_attention_pa_v_kernel(tc, x, w, b, norm_w, y, grad_out, out):
                 multiply(k - 2)
                 for c in range(X_CHUNKS):
                     empty(k - 2, c, nc.scalar.copy)
+            if k + 1 < HEADS:
+                rotate_products(k + 1, (0, 1))
             dots(k)
             if k == 1:
                 quantise_x(3)
-            if k == 0:
-                invert(1)
             if k in (1, 5, 9):
                 invert(k // 4 + 2)
 

@@ -130,32 +130,38 @@ def tile_attention_pa_v_kernel(tc, x, w, b, norm_w, y, grad_out, out):
             )
             if 1 <= level <= 3:
                 coordinate(level - 1)
-        nc.vector.tensor_copy(out=grid[:], in_=grid_int[:])
+        nc.vector.tensor_scalar_mul(out=grid[:], in0=grid_int[:], scalar1=0.5 / math.pi)
+        quarter = keep.tile([P, 1], F32)
+        nc.vector.tensor_scalar_mul(out=quarter[:], in0=frequency[:, 0:1], scalar1=0.5 * math.pi)
 
-        turn = keep.tile([P, 2, PACK, PAIRS], F32)
+        turn = keep.tile([P, PACK, PAIRS], F32)
         nc.vector.tensor_tensor(
-            out=turn[:, 1, :, :PAIRS_T],
+            out=turn[:, :, :PAIRS_T],
             in0=frequency[:, :PAIRS_T].unsqueeze(1).to_broadcast([P, PACK, PAIRS_T]),
             in1=grid[:, 0, :].unsqueeze(2).to_broadcast([P, PACK, PAIRS_T]),
             op=ALU.mult,
         )
         nc.vector.tensor_tensor(
-            out=turn[:, 1, :, PAIRS_T:].rearrange("p j (a k) -> p j a k", a=2),
+            out=turn[:, :, PAIRS_T:].rearrange("p j (a k) -> p j a k", a=2),
             in0=frequency_hw.unsqueeze(1).to_broadcast([P, PACK, 2, PAIRS_HW]),
             in1=grid[:, 1:3, :].rearrange("p a j -> p j a").unsqueeze(3).to_broadcast([P, PACK, 2, PAIRS_HW]),
             op=ALU.mult,
         )
-        nc.vector.tensor_scalar_add(out=turn[:, 0], in0=turn[:, 1], scalar1=0.5 * math.pi)
-        full_turn = keep.tile([P, 2, PACK, PAIRS], F32)
-        nc.vector.tensor_scalar(
-            out=full_turn[:], in0=turn[:], scalar1=math.pi, scalar2=2.0 * math.pi, op0=ALU.is_gt, op1=ALU.mult
-        )
         wrapped = keep.tile([P, 2, PACK, PAIRS], F32)
-        nc.vector.tensor_sub(out=wrapped[:], in0=turn[:], in1=full_turn[:])
+        for k, limit in enumerate((0.25, 0.5)):
+            nc.vector.scalar_tensor_tensor(
+                out=wrapped[:, k].rearrange("p j m -> p (j m)"),
+                in0=turn[:].rearrange("p j m -> p (j m)"),
+                scalar=limit,
+                in1=turn[:].rearrange("p j m -> p (j m)"),
+                op0=ALU.is_gt,
+                op1=ALU.subtract,
+            )
         cos_sin = keep.tile([P, 2, PACK, PAIRS], F32)
 
         def sines():
-            nc.scalar.activation(out=cos_sin[:], in_=wrapped[:], func=ACT.Sin)
+            nc.scalar.activation(out=cos_sin[:, 0], in_=wrapped[:, 0], func=ACT.Sin, scale=-2.0 * math.pi, bias=quarter[:, 0:1])
+            nc.scalar.activation(out=cos_sin[:, 1], in_=wrapped[:, 1], func=ACT.Sin, scale=-2.0 * math.pi)
 
         gains = keep.tile([P, 2, PAIRS, 2], F32)
         gain = psum.tile([P, D], F32, name="acc", bufs=8)

@@ -81,9 +81,9 @@ def tile_attention_pa_v_kernel(tc, x, w, b, norm_w, y, grad_out, out):
         load_g(0)
         load_x(0)
         load_y(1)
+        load_x(1)
         load_g(1)
         load_y(2)
-        load_x(1)
         load_y(3)
         load_x(3)
         load_x(2)
@@ -358,9 +358,9 @@ def tile_attention_pa_v_kernel(tc, x, w, b, norm_w, y, grad_out, out):
                 regroup_x(nc.vector.tensor_copy, 1)
                 invert(1)
             if k == 1:
-                regroup_x(nc.vector.tensor_copy, 3)
                 regroup_x(nc.scalar.copy, 2)
             if k == 2:
+                quantise_x(3)
                 quantise_x(2)
             if k >= 2:
                 quantise_dy(k - 2)
@@ -371,7 +371,7 @@ def tile_attention_pa_v_kernel(tc, x, w, b, norm_w, y, grad_out, out):
                 rotate_products(k + 1, (0, 1))
             dots(k)
             if k == 1:
-                quantise_x(3)
+                regroup_x(nc.vector.tensor_copy, 3)
             if k in (1, 5, 9):
                 invert(k // 4 + 2)
 

@@ -1,6 +1,7 @@
 import math
 
 import concourse.mybir as mybir
+from concourse.masks import make_identity
 
 F32 = mybir.dt.float32
 BF16 = mybir.dt.bfloat16
@@ -31,6 +32,9 @@ BANK = 512
 X_CHUNKS = C // BANK
 GROUPS = ((0, 1), (1, 4), (4, 8), (8, 12), (12, 16))
 GROUP_OF = tuple(i for i, (first, stop) in enumerate(GROUPS) for h in range(first, stop))
+ACC_BANKS = 6
+GPSIMD_TOKENS = 2
+VECTOR_TOKENS = PACK - GPSIMD_TOKENS
 RUN = 4
 
 FLOPS = 2 * TOKENS * E * C
@@ -101,6 +105,8 @@ def tile_attention_pa_v_kernel(tc, x, w, b, norm_w, y, grad_out, out):
         nc.gpsimd.iota(token[:], pattern=[[1, PACK]], base=0, channel_multiplier=PACK)
         ones = keep.tile([P, P], BF16)
         nc.gpsimd.memset(ones[:], 1.0)
+        identity = keep.tile([P, P], BF16)
+        make_identity(nc, identity[:])
         grid_int = keep.tile([P, 3, PACK], I32)
         grid = keep.tile([P, 3, PACK], F32)
 
@@ -164,7 +170,7 @@ def tile_attention_pa_v_kernel(tc, x, w, b, norm_w, y, grad_out, out):
             nc.scalar.activation(out=cos_sin[:, 1], in_=wrapped[:, 1], func=ACT.Sin, scale=-2.0 * math.pi)
 
         gains = keep.tile([P, 2, PAIRS, 2], F32)
-        gain = psum.tile([P, D], F32, name="acc", bufs=8)
+        gain = psum.tile([P, D], F32, name="acc", bufs=ACC_BANKS)
         nc.vector.tensor_copy(out=gain_row[0:1, :], in_=gain_landing[:])
         nc.tensor.matmul(out=gain[:], lhsT=ones[:], rhs=gain_row[:], start=True, stop=True)
         gain_pairs = gain[:].rearrange("p (m e) -> p m e", e=2)
@@ -207,10 +213,6 @@ def tile_attention_pa_v_kernel(tc, x, w, b, norm_w, y, grad_out, out):
             at = (h - GROUPS[i][0]) * D
             return y_group[i][:, j, at : at + D]
 
-        def g_of(h, j):
-            i = GROUP_OF[h]
-            return g_group[i][:, h - GROUPS[i][0], j, :]
-
         def sum_squares(h):
             squares = work.tile([P, PACK, D], F32)
             for j in range(PACK):
@@ -236,6 +238,19 @@ def tile_attention_pa_v_kernel(tc, x, w, b, norm_w, y, grad_out, out):
                 op1=ALU.mult,
             )
 
+        g_bank = {}
+
+        def pass_g(h):
+            i = GROUP_OF[h]
+            g_bank[h] = psum.tile([P, PACK * D], F32, name="g_bank", bufs=2)
+            nc.tensor.matmul(
+                out=g_bank[h][:],
+                lhsT=identity[:],
+                rhs=g_group[i][:, h - GROUPS[i][0]].rearrange("p j d -> p (j d)"),
+                start=True,
+                stop=True,
+            )
+
         products, dn, coefficient, scaled_y, dy_grouped, dy_codes, dy_scales, acc = {}, {}, {}, {}, {}, {}, {}, {}
 
         def rotate_products(h, tokens):
@@ -244,28 +259,35 @@ def tile_attention_pa_v_kernel(tc, x, w, b, norm_w, y, grad_out, out):
             for j in tokens:
                 nc.vector.scalar_tensor_tensor(
                     out=products[h][:, :, j, :],
-                    in0=g_of(h, j).unsqueeze(1).to_broadcast([P, 2, D]),
+                    in0=g_bank[h][:, j * D : (j + 1) * D].unsqueeze(1).to_broadcast([P, 2, D]),
                     scalar=r[:, h, j : j + 1],
                     in1=table[:, :, j, :],
                     op0=ALU.mult,
                     op1=ALU.mult,
                 )
 
-        def rotate_sum(h):
-            dn[h] = work.tile([P, PACK, D], F32, name="dn", bufs=4)
-            nc.vector.tensor_tensor(
-                out=dn[h][:].rearrange("p j (m e) -> p (j m) e", e=2),
-                in0=products[h][:, 0].rearrange("p j (m e) -> p (j m) e", e=2),
-                in1=products[h][:, 1].rearrange("p j (m e) -> p (j m) e", e=2)[:, :, ::-1],
+        def gpsimd_sums(h):
+            return 1 <= h <= HEADS - 2
+
+        def rotate_sum(h, engine, first, stop):
+            if h not in dn:
+                dn[h] = work.tile([P, PACK, D], F32, name="dn", bufs=4)
+            engine.tensor_tensor(
+                out=dn[h][:, first:stop].rearrange("p j (m e) -> p (j m) e", e=2),
+                in0=products[h][:, 0, first:stop].rearrange("p j (m e) -> p (j m) e", e=2),
+                in1=products[h][:, 1, first:stop].rearrange("p j (m e) -> p (j m) e", e=2)[:, :, ::-1],
                 op=ALU.add,
             )
 
         def dots(h):
             coefficient[h] = work.tile([P, PACK], F32, name="coefficient")
-            terms = work.tile([P, PACK, D], F32, name="terms")
+            if gpsimd_sums(h + 1):
+                terms = dn[h + 1][:, VECTOR_TOKENS:]
+            else:
+                terms = work.tile([P, GPSIMD_TOKENS, D], F32, name="terms")
             for j in range(PACK):
                 nc.vector.scalar_tensor_tensor(
-                    out=terms[:, j, :],
+                    out=terms[:, j % GPSIMD_TOKENS, :],
                     in0=dn[h][:, j, :],
                     scalar=pull[:, h, j : j + 1],
                     in1=y_of(h, j),
@@ -306,7 +328,7 @@ def tile_attention_pa_v_kernel(tc, x, w, b, norm_w, y, grad_out, out):
 
         def multiply(h):
             for c in range(X_CHUNKS):
-                acc[h, c] = psum.tile([P, BANK], F32, name="acc", bufs=8)
+                acc[h, c] = psum.tile([P, BANK], F32, name="acc", bufs=ACC_BANKS)
                 nc.tensor.matmul_mx(
                     out=acc[h, c][:],
                     lhsT=dy_codes[h][:].bitcast(E5M2_X4),
@@ -337,16 +359,27 @@ def tile_attention_pa_v_kernel(tc, x, w, b, norm_w, y, grad_out, out):
             sum_squares(h)
         root(2)
 
-        rotate_products(0, (0, 1))
+        ALL = tuple(range(PACK))
+        pass_g(0)
+        pass_g(1)
+        rotate_products(0, ALL)
+        pass_g(2)
+        regroup_x(nc.vector.tensor_copy, 1)
+        rotate_sum(0, nc.vector, 0, PACK)
+        invert(1)
         for k in range(HEADS):
-            rotate_products(k, (2, 3))
             if k >= 1:
                 scale_y(k - 1)
             if k >= 2:
                 project(k - 2)
+            if gpsimd_sums(k):
+                rotate_sum(k, nc.gpsimd, VECTOR_TOKENS, PACK)
+            if k + 1 < HEADS:
+                rotate_products(k + 1, ALL)
+            if k + 3 < HEADS:
+                pass_g(k + 3)
             if k == 1:
                 quantise_x(1)
-            rotate_sum(k)
             if k < 2:
                 sum_squares(8 + 2 * k)
                 sum_squares(9 + 2 * k)
@@ -354,9 +387,6 @@ def tile_attention_pa_v_kernel(tc, x, w, b, norm_w, y, grad_out, out):
                 sum_squares(k // 2 + 11)
             if k in (1, 8):
                 root(k // 8 + 3)
-            if k == 0:
-                regroup_x(nc.vector.tensor_copy, 1)
-                invert(1)
             if k == 1:
                 regroup_x(nc.scalar.copy, 2)
             if k == 2:
@@ -368,12 +398,12 @@ def tile_attention_pa_v_kernel(tc, x, w, b, norm_w, y, grad_out, out):
                 for c in range(X_CHUNKS):
                     empty(k - 2, c, nc.scalar.copy)
             if k + 1 < HEADS:
-                rotate_products(k + 1, (0, 1))
-            dots(k)
+                rotate_sum(k + 1, nc.vector, 0, VECTOR_TOKENS if gpsimd_sums(k + 1) else PACK)
             if k == 1:
                 regroup_x(nc.vector.tensor_copy, 3)
             if k in (1, 5, 9):
                 invert(k // 4 + 2)
+            dots(k)
 
         project(HEADS - 2)
         scale_y(HEADS - 1, on_vector=True)

@@ -33,7 +33,7 @@ X_CHUNKS = C // BANK
 GROUPS = ((0, 1), (1, 4), (4, 8), (8, 12), (12, 16))
 GROUP_OF = tuple(i for i, (first, stop) in enumerate(GROUPS) for h in range(first, stop))
 ACC_BANKS = 6
-GPSIMD_TOKENS = 2
+GPSIMD_TOKENS = 3
 VECTOR_TOKENS = PACK - GPSIMD_TOKENS
 RUN = 4
 

@@ -368,8 +368,6 @@ def tile_attention_pa_v_kernel(tc, x, w, b, norm_w, y, grad_out, out):
         rotate_sum(0, nc.vector, 0, PACK)
         invert(1)
         for k in range(HEADS):
-            if k >= 1:
-                scale_y(k - 1)
             if k >= 2:
                 project(k - 2)
             if gpsimd_sums(k):
@@ -380,13 +378,13 @@ def tile_attention_pa_v_kernel(tc, x, w, b, norm_w, y, grad_out, out):
                 pass_g(k + 3)
             if k == 1:
                 quantise_x(1)
-            if k < 2:
+            if k <= 2:
                 sum_squares(8 + 2 * k)
                 sum_squares(9 + 2 * k)
-            elif k % 2 == 0 and k // 2 + 11 < HEADS:
-                sum_squares(k // 2 + 11)
-            if k in (1, 8):
-                root(k // 8 + 3)
+            elif k in (4, 6):
+                sum_squares(k // 2 + 12)
+            if k in (1, 6):
+                root(k // 6 + 3)
             if k == 1:
                 regroup_x(nc.scalar.copy, 2)
             if k == 2:
@@ -395,8 +393,7 @@ def tile_attention_pa_v_kernel(tc, x, w, b, norm_w, y, grad_out, out):
             if k >= 2:
                 quantise_dy(k - 2)
                 multiply(k - 2)
-                for c in range(X_CHUNKS):
-                    empty(k - 2, c, nc.scalar.copy)
+                empty(k - 2, 0, nc.scalar.copy)
             if k + 1 < HEADS:
                 rotate_sum(k + 1, nc.vector, 0, VECTOR_TOKENS if gpsimd_sums(k + 1) else PACK)
             if k == 1:
@@ -404,6 +401,11 @@ def tile_attention_pa_v_kernel(tc, x, w, b, norm_w, y, grad_out, out):
             if k in (1, 5, 9):
                 invert(k // 4 + 2)
             dots(k)
+            if k + 1 < HEADS:
+                scale_y(k)
+            if k >= 2:
+                for c in range(1, X_CHUNKS):
+                    empty(k - 2, c, nc.scalar.copy)
 
         project(HEADS - 2)
         scale_y(HEADS - 1, on_vector=True)

@@ -33,8 +33,6 @@ X_CHUNKS = C // BANK
 GROUPS = ((0, 1), (1, 4), (4, 8), (8, 12), (12, 16))
 GROUP_OF = tuple(i for i, (first, stop) in enumerate(GROUPS) for h in range(first, stop))
 ACC_BANKS = 6
-GPSIMD_TOKENS = 3
-VECTOR_TOKENS = PACK - GPSIMD_TOKENS
 RUN = 4
 
 FLOPS = 2 * TOKENS * E * C
@@ -269,25 +267,26 @@ def tile_attention_pa_v_kernel(tc, x, w, b, norm_w, y, grad_out, out):
         def gpsimd_sums(h):
             return 1 <= h <= HEADS - 2
 
-        def rotate_sum(h, engine, first, stop):
+        def rotate_sum(h, engine):
             if h not in dn:
                 dn[h] = work.tile([P, PACK, D], F32, name="dn", bufs=4)
             engine.tensor_tensor(
-                out=dn[h][:, first:stop].rearrange("p j (m e) -> p (j m) e", e=2),
-                in0=products[h][:, 0, first:stop].rearrange("p j (m e) -> p (j m) e", e=2),
-                in1=products[h][:, 1, first:stop].rearrange("p j (m e) -> p (j m) e", e=2)[:, :, ::-1],
+                out=dn[h][:].rearrange("p j (m e) -> p (j m) e", e=2),
+                in0=products[h][:, 0].rearrange("p j (m e) -> p (j m) e", e=2),
+                in1=products[h][:, 1].rearrange("p j (m e) -> p (j m) e", e=2)[:, :, ::-1],
                 op=ALU.add,
             )
 
         def dots(h):
             coefficient[h] = work.tile([P, PACK], F32, name="coefficient")
             if gpsimd_sums(h + 1):
-                terms = dn[h + 1][:, VECTOR_TOKENS:]
+                dn[h + 1] = work.tile([P, PACK, D], F32, name="dn", bufs=4)
+                terms = dn[h + 1]
             else:
-                terms = work.tile([P, GPSIMD_TOKENS, D], F32, name="terms")
+                terms = work.tile([P, PACK, D], F32, name="terms")
             for j in range(PACK):
                 nc.vector.scalar_tensor_tensor(
-                    out=terms[:, j % GPSIMD_TOKENS, :],
+                    out=terms[:, j, :],
                     in0=dn[h][:, j, :],
                     scalar=pull[:, h, j : j + 1],
                     in1=y_of(h, j),
@@ -365,13 +364,13 @@ def tile_attention_pa_v_kernel(tc, x, w, b, norm_w, y, grad_out, out):
         rotate_products(0, ALL)
         pass_g(2)
         regroup_x(nc.vector.tensor_copy, 1)
-        rotate_sum(0, nc.vector, 0, PACK)
+        rotate_sum(0, nc.vector)
         invert(1)
         for k in range(HEADS):
             if k >= 2:
                 project(k - 2)
             if gpsimd_sums(k):
-                rotate_sum(k, nc.gpsimd, VECTOR_TOKENS, PACK)
+                rotate_sum(k, nc.gpsimd)
             if k + 1 < HEADS:
                 rotate_products(k + 1, ALL)
             if k + 3 < HEADS:
@@ -394,8 +393,8 @@ def tile_attention_pa_v_kernel(tc, x, w, b, norm_w, y, grad_out, out):
                 quantise_dy(k - 2)
                 multiply(k - 2)
                 empty(k - 2, 0, nc.scalar.copy)
-            if k + 1 < HEADS:
-                rotate_sum(k + 1, nc.vector, 0, VECTOR_TOKENS if gpsimd_sums(k + 1) else PACK)
+            if k + 1 == HEADS - 1:
+                rotate_sum(k + 1, nc.vector)
             if k == 1:
                 regroup_x(nc.vector.tensor_copy, 3)
             if k in (1, 5, 9):

@@ -295,9 +295,13 @@ def tile_attention_pa_v_kernel(tc, x, w, b, norm_w, y, grad_out, out):
                     accum_out=coefficient[h][:, j : j + 1],
                 )
 
-        def scale_y(h, on_vector=False):
-            scaled_y[h] = work.tile([P, PACK, D], F32, name="scaled_y")
-            for j in range(PACK):
+        def scalar_tokens(h):
+            return 0 if h >= HEADS - 2 else PACK - h % 2
+
+        def scale_y(h, on_vector):
+            if h not in scaled_y:
+                scaled_y[h] = work.tile([P, PACK, D], F32, name="scaled_y")
+            for j in range(scalar_tokens(h), PACK) if on_vector else range(scalar_tokens(h)):
                 if on_vector:
                     nc.vector.tensor_scalar_mul(
                         out=scaled_y[h][:, j, :], in0=y_of(h, j), scalar1=coefficient[h][:, j : j + 1]
@@ -375,6 +379,8 @@ def tile_attention_pa_v_kernel(tc, x, w, b, norm_w, y, grad_out, out):
                 rotate_products(k + 1, ALL)
             if k + 3 < HEADS:
                 pass_g(k + 3)
+            if k >= 1:
+                scale_y(k - 1, on_vector=True)
             if k == 1:
                 quantise_x(1)
             if k <= 2:
@@ -400,8 +406,7 @@ def tile_attention_pa_v_kernel(tc, x, w, b, norm_w, y, grad_out, out):
             if k in (1, 5, 9):
                 invert(k // 4 + 2)
             dots(k)
-            if k + 1 < HEADS:
-                scale_y(k)
+            scale_y(k, on_vector=False)
             if k >= 2:
                 for c in range(1, X_CHUNKS):
                     empty(k - 2, c, nc.scalar.copy)

@@ -175,9 +175,9 @@ def tile_attention_pa_v_kernel(tc, x, w, b, norm_w, y, grad_out, out):
         table = keep.tile([P, 2, PACK, D], F32)
 
         def sort_gains():
-            nc.vector.tensor_copy(out=gains[:, 0], in_=gain_pairs)
-            nc.vector.tensor_copy(out=gains[:, 1, :, 1], in_=gain_pairs[:, :, 0])
-            nc.vector.tensor_scalar_mul(out=gains[:, 1, :, 0], in0=gain_pairs[:, :, 1], scalar1=-1.0)
+            nc.scalar.copy(out=gains[:, 0], in_=gain_pairs)
+            nc.scalar.copy(out=gains[:, 1, :, 1], in_=gain_pairs[:, :, 0])
+            nc.scalar.activation(out=gains[:, 1, :, 0], in_=gain_pairs[:, :, 1], func=ACT.Copy, scale=-1.0)
 
         def build_table():
             nc.vector.tensor_tensor(
@@ -202,7 +202,6 @@ def tile_attention_pa_v_kernel(tc, x, w, b, norm_w, y, grad_out, out):
             )
 
         square_sum = keep.tile([P, HEADS, PACK], F32)
-        rms = keep.tile([P, HEADS, PACK], F32)
         r = keep.tile([P, HEADS, PACK], F32)
         pull = keep.tile([P, HEADS, PACK], F32)
 
@@ -221,12 +220,15 @@ def tile_attention_pa_v_kernel(tc, x, w, b, norm_w, y, grad_out, out):
         def root(i):
             first, stop = GROUPS[i]
             nc.scalar.activation(
-                out=rms[:, first:stop, :], in_=square_sum[:, first:stop, :], func=ACT.Sqrt, scale=1.0 / D, bias=eps[:, 0:1]
+                out=r[:, first:stop, :],
+                in_=square_sum[:, first:stop, :],
+                func=ACT.Abs_reciprocal_sqrt,
+                scale=1.0 / D,
+                bias=eps[:, 0:1],
             )
 
         def invert(i):
             first, stop = GROUPS[i]
-            nc.vector.reciprocal(out=r[:, first:stop, :], in_=rms[:, first:stop, :])
             nc.vector.scalar_tensor_tensor(
                 out=pull[:, first:stop, :],
                 in0=r[:, first:stop, :],
@@ -349,11 +351,11 @@ def tile_attention_pa_v_kernel(tc, x, w, b, norm_w, y, grad_out, out):
 
         sum_squares(0)
         sines()
+        sort_gains()
         root(0)
         regroup_x(nc.vector.tensor_copy, 0)
-        sort_gains()
-        quantise_x(0)
         build_table()
+        quantise_x(0)
         invert(0)
         for h in range(1, 4):
             sum_squares(h)

import math

import concourse.mybir as mybir
from concourse.masks import make_identity

F32 = mybir.dt.float32
BF16 = mybir.dt.bfloat16
I32 = mybir.dt.int32
U32 = mybir.dt.uint32
U8 = mybir.dt.uint8
E4M3_X4 = mybir.dt.float8_e4m3fn_x4
E5M2_X4 = mybir.dt.float8_e5m2_x4
ALU = mybir.AluOpType
ACT = mybir.ActivationFunctionType

P = 128
PACK = 4
TOKENS = P * PACK
HEADS = 16
D = 128
PAIRS = D // 2
E = HEADS * D
C = 2048
EPS = 1e-6
BASE = 10000.0
DIM_T = D - 4 * (D // 6)
DIM_HW = 2 * (D // 6)
PAIRS_T = DIM_T // 2
PAIRS_HW = DIM_HW // 2

BANK = 512
X_CHUNKS = C // BANK
GROUPS = ((0, 1), (1, 4), (4, 8), (8, 12), (12, 16))
GROUP_OF = tuple(i for i, (first, stop) in enumerate(GROUPS) for h in range(first, stop))
ACC_BANKS = 6
RUN = 4

FLOPS = 2 * TOKENS * E * C
BYTES = 2 * TOKENS * C + 2 * D + 4 * TOKENS * E + 2 * TOKENS * E + 4 * E * C


def regroup(copy, grouped, rows):
    copy(
        out=grouped.rearrange("p (c i) j -> p c j i", i=RUN),
        in_=rows.rearrange("p j (c i) -> p c j i", i=RUN),
    )


def tile_attention_pa_v_kernel(tc, x, w, b, norm_w, y, grad_out, out):
    nc = tc.nc
    x_rows = x.flatten_outer_dims().rearrange("(p j) c -> p j c", j=PACK)
    y_rows = y.flatten_outer_dims().rearrange("(p j) e -> p j e", j=PACK)
    g_rows = grad_out.flatten_outer_dims().rearrange("(h p j) d -> p h (j d)", h=HEADS, j=PACK)

    with tc.tile_pool(name="keep", bufs=1) as keep, tc.tile_pool(name="work", bufs=3) as work, tc.psum_pool(
        name="psum", bufs=2
    ) as psum, tc.manual_schedule():
        gain_landing = keep.tile([1, D], BF16)
        nc.scalar.dma_start(out=gain_landing[:], in_=norm_w.unsqueeze(0))
        gain_row = keep.tile([P, D], BF16)
        nc.vector.memset(gain_row[:], 0.0)

        x_raw = [keep.tile([P, PACK, BANK], BF16, name="x_raw%d" % c) for c in range(X_CHUNKS)]
        y_group = [
            keep.tile([P, PACK, (stop - first) * D], F32, name="y_group%d" % i) for i, (first, stop) in enumerate(GROUPS)
        ]
        g_group = [
            keep.tile([P, stop - first, PACK, D], BF16, name="g_group%d" % i) for i, (first, stop) in enumerate(GROUPS)
        ]

        def load_x(c):
            nc.sync.dma_start(out=x_raw[c][:], in_=x_rows[:, :, c * BANK : (c + 1) * BANK])

        def load_y(i):
            first, stop = GROUPS[i]
            nc.sync.dma_start(out=y_group[i][:], in_=y_rows[:, :, first * D : stop * D])

        def load_g(i):
            first, stop = GROUPS[i]
            nc.sync.dma_start(out=g_group[i][:].rearrange("p h j d -> p h (j d)"), in_=g_rows[:, first:stop, :])

        load_y(0)
        load_g(0)
        load_x(0)
        load_y(1)
        load_x(1)
        load_g(1)
        load_y(2)
        load_y(3)
        load_x(3)
        load_x(2)
        load_g(2)
        load_y(4)
        load_g(3)
        load_g(4)

        eps = keep.tile([P, 1], F32)
        nc.vector.memset(eps[:], EPS)
        warm = keep.tile([P, 1], F32)
        nc.scalar.activation(out=warm[:], in_=eps[:], func=ACT.Sin)

        token = keep.tile([P, PACK], I32)
        nc.gpsimd.iota(token[:], pattern=[[1, PACK]], base=0, channel_multiplier=PACK)
        ones = keep.tile([P, P], BF16)
        nc.gpsimd.memset(ones[:], 1.0)
        identity = keep.tile([P, P], BF16)
        make_identity(nc, identity[:])
        grid_int = keep.tile([P, 3, PACK], I32)
        grid = keep.tile([P, 3, PACK], F32)

        def coordinate(a):
            nc.vector.tensor_scalar(
                out=grid_int[:, a, :],
                in0=token[:],
                scalar1=6 - 3 * a,
                scalar2=7,
                op0=ALU.arith_shift_right,
                op1=ALU.bitwise_and,
            )

        frequency = keep.tile([P, PAIRS], F32)
        nc.vector.memset(frequency[:], 1.0)
        frequency_hw = frequency[:, PAIRS_T:].rearrange("p (a k) -> p a k", a=2)
        for level, n in enumerate((1, 2, 4, 8, 16)):
            nc.vector.tensor_scalar_mul(
                out=frequency[:, n : min(2 * n, PAIRS_T)],
                in0=frequency[:, 0 : min(n, PAIRS_T - n)],
                scalar1=BASE ** (-2.0 * n / DIM_T),
            )
            nc.vector.tensor_scalar_mul(
                out=frequency_hw[:, :, n : min(2 * n, PAIRS_HW)],
                in0=frequency_hw[:, :, 0 : min(n, PAIRS_HW - n)],
                scalar1=BASE ** (-2.0 * n / DIM_HW),
            )
            if 1 <= level <= 3:
                coordinate(level - 1)
        nc.vector.tensor_scalar_mul(out=grid[:], in0=grid_int[:], scalar1=0.5 / math.pi)
        quarter = keep.tile([P, 1], F32)
        nc.vector.tensor_scalar_mul(out=quarter[:], in0=frequency[:, 0:1], scalar1=0.5 * math.pi)

        turn = keep.tile([P, PACK, PAIRS], F32)
        nc.vector.tensor_tensor(
            out=turn[:, :, :PAIRS_T],
            in0=frequency[:, :PAIRS_T].unsqueeze(1).to_broadcast([P, PACK, PAIRS_T]),
            in1=grid[:, 0, :].unsqueeze(2).to_broadcast([P, PACK, PAIRS_T]),
            op=ALU.mult,
        )
        nc.vector.tensor_tensor(
            out=turn[:, :, PAIRS_T:].rearrange("p j (a k) -> p j a k", a=2),
            in0=frequency_hw.unsqueeze(1).to_broadcast([P, PACK, 2, PAIRS_HW]),
            in1=grid[:, 1:3, :].rearrange("p a j -> p j a").unsqueeze(3).to_broadcast([P, PACK, 2, PAIRS_HW]),
            op=ALU.mult,
        )
        wrapped = keep.tile([P, 2, PACK, PAIRS], F32)
        for k, limit in enumerate((0.25, 0.5)):
            nc.vector.scalar_tensor_tensor(
                out=wrapped[:, k].rearrange("p j m -> p (j m)"),
                in0=turn[:].rearrange("p j m -> p (j m)"),
                scalar=limit,
                in1=turn[:].rearrange("p j m -> p (j m)"),
                op0=ALU.is_gt,
                op1=ALU.subtract,
            )
        cos_sin = keep.tile([P, 2, PACK, PAIRS], F32)

        def sines():
            nc.scalar.activation(out=cos_sin[:, 0], in_=wrapped[:, 0], func=ACT.Sin, scale=-2.0 * math.pi, bias=quarter[:, 0:1])
            nc.scalar.activation(out=cos_sin[:, 1], in_=wrapped[:, 1], func=ACT.Sin, scale=-2.0 * math.pi)

        gains = keep.tile([P, 2, PAIRS, 2], F32)
        gain = psum.tile([P, D], F32, name="acc", bufs=ACC_BANKS)
        nc.vector.tensor_copy(out=gain_row[0:1, :], in_=gain_landing[:])
        nc.tensor.matmul(out=gain[:], lhsT=ones[:], rhs=gain_row[:], start=True, stop=True)
        gain_pairs = gain[:].rearrange("p (m e) -> p m e", e=2)
        table = keep.tile([P, 2, PACK, D], F32)

        def sort_gains():
            nc.scalar.copy(out=gains[:, 0], in_=gain_pairs)
            nc.scalar.copy(out=gains[:, 1, :, 1], in_=gain_pairs[:, :, 0])
            nc.scalar.activation(out=gains[:, 1, :, 0], in_=gain_pairs[:, :, 1], func=ACT.Copy, scale=-1.0)

        def build_table():
            nc.vector.tensor_tensor(
                out=table[:].rearrange("p k j (m e) -> p k j m e", e=2),
                in0=cos_sin[:].unsqueeze(4).to_broadcast([P, 2, PACK, PAIRS, 2]),
                in1=gains[:].unsqueeze(2).to_broadcast([P, 2, PACK, PAIRS, 2]),
                op=ALU.mult,
            )

        x_grouped = [keep.tile([P, BANK, PACK], BF16, name="x_grouped%d" % c, align_bytes=64) for c in range(X_CHUNKS)]
        x_codes = [keep.tile([P, BANK], U32, name="x_codes%d" % c, align_bytes=64) for c in range(X_CHUNKS)]
        x_scales = [keep.tile([P, BANK], U8, name="x_scales%d" % c, align_bytes=64) for c in range(X_CHUNKS)]

        def regroup_x(copy, c):
            regroup(copy, x_grouped[c][:], x_raw[c][:])

        def quantise_x(c):
            nc.vector.quantize_mx(
                out=x_codes[c][:].bitcast(E4M3_X4),
                scales=x_scales[c][:],
                in_=x_grouped[c][:].rearrange("p c j -> p (c j)"),
            )

        square_sum = keep.tile([P, HEADS, PACK], F32)
        r = keep.tile([P, HEADS, PACK], F32)
        pull = keep.tile([P, HEADS, PACK], F32)

        def y_of(h, j):
            i = GROUP_OF[h]
            at = (h - GROUPS[i][0]) * D
            return y_group[i][:, j, at : at + D]

        def sum_squares(h):
            squares = work.tile([P, PACK, D], F32)
            for j in range(PACK):
                nc.scalar.activation(
                    out=squares[:, j, :], in_=y_of(h, j), func=ACT.Square, accum_out=square_sum[:, h, j : j + 1]
                )

        def root(i):
            first, stop = GROUPS[i]
            nc.scalar.activation(
                out=r[:, first:stop, :],
                in_=square_sum[:, first:stop, :],
                func=ACT.Abs_reciprocal_sqrt,
                scale=1.0 / D,
                bias=eps[:, 0:1],
            )

        def invert(i):
            first, stop = GROUPS[i]
            nc.vector.scalar_tensor_tensor(
                out=pull[:, first:stop, :],
                in0=r[:, first:stop, :],
                scalar=-1.0 / D,
                in1=r[:, first:stop, :],
                op0=ALU.mult,
                op1=ALU.mult,
            )

        g_bank = {}

        def pass_g(h):
            i = GROUP_OF[h]
            g_bank[h] = psum.tile([P, PACK * D], F32, name="g_bank", bufs=2)
            nc.tensor.matmul(
                out=g_bank[h][:],
                lhsT=identity[:],
                rhs=g_group[i][:, h - GROUPS[i][0]].rearrange("p j d -> p (j d)"),
                start=True,
                stop=True,
            )

        products, dn, coefficient, scaled_y, dy_grouped, dy_codes, dy_scales, acc = {}, {}, {}, {}, {}, {}, {}, {}

        def rotate_products(h, tokens):
            if h not in products:
                products[h] = work.tile([P, 2, PACK, D], F32, name="products")
            for j in tokens:
                nc.vector.scalar_tensor_tensor(
                    out=products[h][:, :, j, :],
                    in0=g_bank[h][:, j * D : (j + 1) * D].unsqueeze(1).to_broadcast([P, 2, D]),
                    scalar=r[:, h, j : j + 1],
                    in1=table[:, :, j, :],
                    op0=ALU.mult,
                    op1=ALU.mult,
                )

        def gpsimd_sums(h):
            return 1 <= h <= HEADS - 2

        def rotate_sum(h, engine):
            if h not in dn:
                dn[h] = work.tile([P, PACK, D], F32, name="dn", bufs=4)
            engine.tensor_tensor(
                out=dn[h][:].rearrange("p j (m e) -> p (j m) e", e=2),
                in0=products[h][:, 0].rearrange("p j (m e) -> p (j m) e", e=2),
                in1=products[h][:, 1].rearrange("p j (m e) -> p (j m) e", e=2)[:, :, ::-1],
                op=ALU.add,
            )

        def dots(h):
            coefficient[h] = work.tile([P, PACK], F32, name="coefficient")
            if gpsimd_sums(h + 1):
                dn[h + 1] = work.tile([P, PACK, D], F32, name="dn", bufs=4)
                terms = dn[h + 1]
            else:
                terms = work.tile([P, PACK, D], F32, name="terms")
            for j in range(PACK):
                nc.vector.scalar_tensor_tensor(
                    out=terms[:, j, :],
                    in0=dn[h][:, j, :],
                    scalar=pull[:, h, j : j + 1],
                    in1=y_of(h, j),
                    op0=ALU.mult,
                    op1=ALU.mult,
                    accum_out=coefficient[h][:, j : j + 1],
                )

        def scalar_tokens(h):
            return 0 if h >= HEADS - 2 else PACK - h % 2

        def scale_y(h, on_vector):
            if h not in scaled_y:
                scaled_y[h] = work.tile([P, PACK, D], F32, name="scaled_y")
            for j in range(scalar_tokens(h), PACK) if on_vector else range(scalar_tokens(h)):
                if on_vector:
                    nc.vector.tensor_scalar_mul(
                        out=scaled_y[h][:, j, :], in0=y_of(h, j), scalar1=coefficient[h][:, j : j + 1]
                    )
                else:
                    nc.scalar.activation(
                        out=scaled_y[h][:, j, :], in_=y_of(h, j), func=ACT.Copy, scale=coefficient[h][:, j : j + 1]
                    )

        def project(h):
            dy_grouped[h] = work.tile([P, D, PACK], BF16, name="dy_grouped", align_bytes=64)
            nc.vector.tensor_tensor(
                out=dy_grouped[h][:].rearrange("p (c i) j -> p c j i", i=RUN),
                in0=dn[h][:].rearrange("p j (c i) -> p c j i", i=RUN),
                in1=scaled_y[h][:].rearrange("p j (c i) -> p c j i", i=RUN),
                op=ALU.add,
            )

        def quantise_dy(h):
            dy_codes[h] = work.tile([P, D], U32, name="dy_codes", align_bytes=64)
            dy_scales[h] = work.tile([P, D], U8, name="dy_scales", align_bytes=64)
            nc.vector.quantize_mx(
                out=dy_codes[h][:].bitcast(E5M2_X4),
                scales=dy_scales[h][:],
                in_=dy_grouped[h][:].rearrange("p d j -> p (d j)"),
            )

        def multiply(h):
            for c in range(X_CHUNKS):
                acc[h, c] = psum.tile([P, BANK], F32, name="acc", bufs=ACC_BANKS)
                nc.tensor.matmul_mx(
                    out=acc[h, c][:],
                    lhsT=dy_codes[h][:].bitcast(E5M2_X4),
                    lhsT_scale=dy_scales[h][:],
                    rhs=x_codes[c][:].bitcast(E4M3_X4),
                    rhs_scale=x_scales[c][:],
                    start=True,
                    stop=True,
                )

        def empty(h, c, copy):
            result = work.tile([P, BANK], F32, name="result", bufs=8)
            copy(out=result[:], in_=acc[h, c][:])
            nc.sync.dma_start(out=out[h * D : (h + 1) * D, c * BANK : (c + 1) * BANK], in_=result[:])

        sum_squares(0)
        sines()
        sort_gains()
        root(0)
        regroup_x(nc.vector.tensor_copy, 0)
        build_table()
        quantise_x(0)
        invert(0)
        for h in range(1, 4):
            sum_squares(h)
        root(1)
        for h in range(4, 8):
            sum_squares(h)
        root(2)

        ALL = tuple(range(PACK))
        pass_g(0)
        pass_g(1)
        rotate_products(0, ALL)
        pass_g(2)
        regroup_x(nc.vector.tensor_copy, 1)
        rotate_sum(0, nc.vector)
        invert(1)
        for k in range(HEADS):
            if k >= 2:
                project(k - 2)
            if gpsimd_sums(k):
                rotate_sum(k, nc.gpsimd)
            if k + 1 < HEADS:
                rotate_products(k + 1, ALL)
            if k + 3 < HEADS:
                pass_g(k + 3)
            if k >= 1:
                scale_y(k - 1, on_vector=True)
            if k == 1:
                quantise_x(1)
            if k <= 2:
                sum_squares(8 + 2 * k)
                sum_squares(9 + 2 * k)
            elif k in (4, 6):
                sum_squares(k // 2 + 12)
            if k in (1, 6):
                root(k // 6 + 3)
            if k == 1:
                regroup_x(nc.scalar.copy, 2)
            if k == 2:
                quantise_x(3)
                quantise_x(2)
            if k >= 2:
                quantise_dy(k - 2)
                multiply(k - 2)
                empty(k - 2, 0, nc.scalar.copy)
            if k + 1 == HEADS - 1:
                rotate_sum(k + 1, nc.vector)
            if k == 1:
                regroup_x(nc.vector.tensor_copy, 3)
            if k in (1, 5, 9):
                invert(k // 4 + 2)
            dots(k)
            scale_y(k, on_vector=False)
            if k >= 2:
                for c in range(1, X_CHUNKS):
                    empty(k - 2, c, nc.scalar.copy)

        project(HEADS - 2)
        scale_y(HEADS - 1, on_vector=True)
        quantise_dy(HEADS - 2)
        multiply(HEADS - 2)
        project(HEADS - 1)
        empty(HEADS - 2, 0, nc.scalar.copy)
        empty(HEADS - 2, 1, nc.scalar.copy)
        quantise_dy(HEADS - 1)
        multiply(HEADS - 1)
        empty(HEADS - 2, 2, nc.vector.tensor_copy)
        empty(HEADS - 2, 3, nc.vector.tensor_copy)
        for c in range(X_CHUNKS):
            empty(HEADS - 1, c, nc.vector.tensor_copy if c % 2 == 1 else nc.scalar.copy)
